import numpy as np
import ml_dtypes


def mxq(x, axis, fmt="e4m3"):
    dtype, down = {"e4m3": (ml_dtypes.float8_e4m3fn, 7), "e5m2": (ml_dtypes.float8_e5m2, 14)}[fmt]
    v = np.moveaxis(np.asarray(x, np.float32).astype(ml_dtypes.bfloat16).astype(np.float64), axis, -1)
    blocks = v.reshape(v.shape[:-1] + (-1, 32))
    amax = np.abs(blocks).max(-1, keepdims=True)
    byte = np.maximum(np.where(amax > 0, np.frexp(amax)[1] - 1 + 127, 0) - down, 1)
    scale = np.exp2(byte - 127.0)
    codes = (blocks / scale).astype(np.float32).astype(dtype).astype(np.float64)
    return np.moveaxis((codes * scale).reshape(v.shape), -1, axis)


WIDE = False


def mx_kscale(k):
    if not WIDE:
        return np.ones(k)
    levels = np.array([10, -10, 5, -5, 0])
    a = np.random.permutation(np.resize(levels, k // 512 * 4)).reshape(k // 512, 4)
    idx = np.arange(k)
    return np.exp2(a[idx // 512, idx % 128 // 32])


BF16 = ml_dtypes.bfloat16


def bf(x):
    return np.asarray(x, np.float32).astype(BF16)


def f64(x):
    return np.asarray(x).astype(np.float64)


B, D, E, H, L = 512, 512, 16, 512, 128
NOISE_EPS = 0.01
MEAN_EPS = 1e-8


def softplus(z):
    return np.log(1.0 + np.exp(z))


def noisy_gates(clean_logits, noise_pre, noise):
    sd = softplus(noise_pre) + NOISE_EPS
    l = clean_logits + noise * sd
    e = np.exp(l - l.max(1, keepdims=True))
    p = e / e.sum(1, keepdims=True)
    m = p.mean(-1) - MEAN_EPS
    g = np.where(p >= m[:, None], p, 0.0)
    return g / g.sum(-1, keepdims=True)


def setup_inputs():
    s = mx_kscale(D)
    return {"x": bf(np.random.standard_normal((B, D)) * s),
            "noise": bf(np.random.standard_normal((B, E))),
            "clean_logits": bf(np.random.standard_normal((B, E))),
            "noise_pre": bf(np.random.standard_normal((B, E))),
            "W1": bf(np.random.standard_normal((E, D, H)) / np.sqrt(D) / s[None, :, None]),
            "b1": bf(np.random.standard_normal((E, H)) * 0.2),
            "W2": bf(np.random.standard_normal((E, H, L)) * 2.0 / np.sqrt(H)),
            "b2": bf(np.random.standard_normal((E, L)) * 0.3)}


def reference(x, noise, clean_logits, noise_pre, W1, b1, W2, b2):
    gates = noisy_gates(f64(clean_logits), f64(noise_pre), f64(noise))
    h = np.tanh((mxq(f64(x), 1, "e4m3") @ mxq(f64(W1), 1, "e4m3")) + f64(b1)[:, None, :])
    y = (mxq(h, 2, "e4m3") @ mxq(f64(W2), 1, "e4m3")) + f64(b2)[:, None, :]
    return gates[:, :, None] * y.transpose(1, 0, 2)

@@ -1,0 +1,307 @@
+from contextlib import ExitStack
+
+import concourse.mybir as mybir
+from concourse.masks import make_identity
+
+F32 = mybir.dt.float32
+BF16 = mybir.dt.bfloat16
+U32 = mybir.dt.uint32
+U8 = mybir.dt.uint8
+FP8X4 = mybir.dt.float8_e4m3fn_x4
+ACT = mybir.ActivationFunctionType
+ALU = mybir.AluOpType
+AX = mybir.AxisListType
+
+P = 128
+B, D, E, H, L = 512, 512, 16, 512, 128
+NB = B // P
+FLOPS = 2 * E * B * D * H + 2 * E * B * H * L
+
+SC_GROUPS = 56
+
+
+def tile_mblfe_pa_kernel(tc, x, noise, clean_logits, noise_pre, W1, b1, W2, b2, out):
+    nc = tc.nc
+    with ExitStack() as ctx:
+        keep = ctx.enter_context(tc.tile_pool(name="keep", bufs=1))
+        rot = ctx.enter_context(tc.tile_pool(name="rot", bufs=3))
+        ps1 = ctx.enter_context(tc.psum_pool(name="ps1", bufs=6))
+        ps2 = ctx.enter_context(tc.psum_pool(name="ps2", bufs=2))
+
+        x_sb = keep.tile([P, NB * D], BF16, name="x_sb", align_bytes=64)
+        nc.sync.dma_start(out=x_sb[:], in_=x.rearrange("(p n) d -> p (n d)", n=NB))
+        w1raw = []
+        for e in range(E):
+            w1raw.append(keep.tile([P, 4 * H], BF16, name="w1raw%d" % e, align_bytes=64))
+        w2raw = keep.tile([P, E * 4 * L], BF16, name="w2raw", align_bytes=64)
+        b2b = keep.tile([P, E * L], BF16, name="b2b", align_bytes=64)
+
+        def load_w1(e):
+            nc.sync.dma_start(out=w1raw[e][:], in_=W1[e].rearrange("(p j) h -> p (j h)", j=4))
+
+        def load_w2(q):
+            nc.sync.dma_start(
+                out=w2raw[:, q * 2048 : (q + 1) * 2048].rearrange("p (e t l) -> p e t l", e=4, t=4),
+                in_=W2[4 * q : 4 * q + 4].rearrange("e (t p) l -> p e t l", p=P),
+            )
+
+        np_in = keep.tile([P, NB * E], BF16, name="np_in")
+        no_in = keep.tile([P, NB * E], BF16, name="no_in")
+        cl_in = keep.tile([P, NB * E], BF16, name="cl_in")
+        nc.scalar.dma_start(out=np_in[:], in_=noise_pre.rearrange("(p n) e -> p (n e)", n=NB))
+        nc.scalar.dma_start(out=no_in[:], in_=noise.rearrange("(p n) e -> p (n e)", n=NB))
+        nc.scalar.dma_start(out=cl_in[:], in_=clean_logits.rearrange("(p n) e -> p (n e)", n=NB))
+        b1raw = keep.tile([P, P], BF16, name="b1raw")
+        nc.vector.memset(b1raw[:], 0.0)
+        nc.scalar.dma_start(out=b1raw[0:64, :], in_=b1.rearrange("e (t p) -> (e t) p", p=P))
+
+        load_w1(0)
+        load_w1(1)
+        load_w2(0)
+        load_w1(2)
+        load_w1(3)
+        nc.sync.dma_start(out=b2b[:], in_=b2.rearrange("e l -> (e l)").partition_broadcast(P))
+        for e in range(4, E):
+            load_w1(e)
+            if e % 4 == 0:
+                load_w2(e // 4)
+
+        ident = keep.tile([P, P], F32, name="ident")
+        make_identity(nc, ident[:])
+
+        x32 = x_sb[:].bitcast(F32).rearrange("p (n q u) -> p n u q", n=NB, u=2)
+        gx = keep.tile([P, 4 * B], BF16, name="gx", align_bytes=64)
+        gx32 = gx[:].bitcast(F32)
+        xc = keep.tile([P, B], U32, name="xc", align_bytes=64)
+        xs = keep.tile([P, B], U8, name="xs", align_bytes=64)
+        for half in range(2):
+            xt = ps1.tile([P, 512], F32, name="xt", tag="s1")
+            for m in range(2):
+                for u in range(2):
+                    nc.tensor.transpose(
+                        out=xt[:, (2 * m + u) * P : (2 * m + u + 1) * P],
+                        in_=x32[:, 2 * half + m, u, :],
+                        identity=ident[:],
+                    )
+            dst = gx32[:, half * 512 : (half + 1) * 512].rearrange("p (m b u) -> p m b u", m=2, u=2)
+            src = xt[:].rearrange("p (m u b) -> p m b u", m=2, u=2)
+            if half == 0:
+                nc.vector.tensor_copy(out=dst, in_=src)
+            else:
+                nc.scalar.copy(out=dst, in_=src)
+        nc.vector.quantize_mx(out=xc[:].bitcast(FP8X4), scales=xs[:], in_=gx[:])
+
+        b1f = keep.tile([P, P], F32, name="b1f")
+        nc.vector.tensor_copy(out=b1f[:], in_=b1raw[:])
+        pb = ps2.tile([P, 512], F32, name="pb", tag="s2")
+        nc.tensor.transpose(out=pb[:, 0:P], in_=b1f[:], identity=ident[:])
+        b1T = keep.tile([P, 4 * E], F32, name="b1T")
+        nc.vector.tensor_copy(out=b1T[:], in_=pb[:, 0 : 4 * E])
+
+        def gt(name, w=NB * E):
+            return keep.tile([P, w], F32, name=name)
+
+        def v3(t):
+            return t[:].rearrange("p (n e) -> p n e", n=NB)
+
+        def bc(t):
+            return t[:].unsqueeze(2).to_broadcast([P, NB, E])
+
+        nabs = gt("nabs")
+        nc.vector.scalar_tensor_tensor(out=nabs[:], in0=np_in[:], scalar=-1.0, in1=np_in[:], op0=ALU.mult, op1=ALU.min)
+        eu = gt("eu")
+        nc.scalar.activation(out=eu[:], in_=nabs[:], func=ACT.Exp)
+        lg = gt("lg")
+        nc.scalar.activation(out=lg[:], in_=eu[:], func=ACT.Ln, bias=1.0, scale=1.0)
+        sp = gt("sp")
+        nc.vector.scalar_tensor_tensor(out=sp[:], in0=np_in[:], scalar=0.0, in1=lg[:], op0=ALU.max, op1=ALU.add)
+        nz = gt("nz")
+        nc.vector.scalar_tensor_tensor(out=nz[:], in0=sp[:], scalar=0.01, in1=no_in[:], op0=ALU.add, op1=ALU.mult)
+        lo = gt("lo")
+        nc.vector.tensor_tensor(out=lo[:], in0=nz[:], in1=cl_in[:], op=ALU.add)
+        mx = gt("mx", NB)
+        nc.vector.tensor_reduce(out=mx[:], in_=v3(lo), axis=AX.X, op=ALU.max)
+        ls = gt("ls")
+        nc.vector.tensor_tensor(out=v3(ls), in0=v3(lo), in1=bc(mx), op=ALU.subtract)
+        ex = gt("ex")
+        nc.scalar.activation(out=ex[:], in_=ls[:], func=ACT.Exp)
+        sm = gt("sm", NB)
+        nc.vector.tensor_reduce(out=sm[:], in_=v3(ex), axis=AX.X, op=ALU.add)
+        rs = gt("rs", NB)
+        nc.vector.reciprocal(out=rs[:], in_=sm[:])
+        pr = gt("pr")
+        nc.vector.tensor_tensor(out=v3(pr), in0=v3(ex), in1=bc(rs), op=ALU.mult)
+        pm = gt("pm", NB)
+        nc.vector.tensor_reduce(out=pm[:], in_=v3(pr), axis=AX.X, op=ALU.add)
+        th = gt("th", NB)
+        nc.vector.tensor_scalar(out=th[:], in0=pm[:], scalar1=1.0 / E, scalar2=-1e-8, op0=ALU.mult, op1=ALU.add)
+        mk = gt("mk")
+        nc.vector.tensor_tensor(out=v3(mk), in0=v3(pr), in1=bc(th), op=ALU.is_ge)
+        gq = gt("gq")
+        nc.vector.tensor_tensor(out=gq[:], in0=pr[:], in1=mk[:], op=ALU.mult)
+        gs = gt("gs", NB)
+        nc.vector.tensor_reduce(out=gs[:], in_=v3(gq), axis=AX.X, op=ALU.add)
+        rg = gt("rg", NB)
+        nc.vector.reciprocal(out=rg[:], in_=gs[:])
+        g = gt("g")
+        nc.vector.tensor_tensor(out=v3(g), in0=v3(gq), in1=bc(rg), op=ALU.mult)
+
+        o = keep.tile([P, NB * E * L], F32, name="o")
+        o3 = o[:].rearrange("p (n c) -> p n c", n=NB)
+        out_v = out.rearrange("(p n) e l -> p n (e l)", n=NB)
+        w2c = keep.tile([P, E * L], U32, name="w2c", align_bytes=64)
+        w2s = keep.tile([P, E * L], U8, name="w2s", align_bytes=64)
+
+        def views(dst2d, src2d):
+            src = src2d.rearrange("p (j c i) -> p c j i", j=4, i=4)
+            dst = dst2d.rearrange("p (c i j) -> p c j i", i=4, j=4)
+            return dst, src
+
+        g1 = {}
+        w1c = {}
+        w1s = {}
+        g3 = {}
+        hT = {}
+        g2 = {}
+        hc = {}
+        hs = {}
+        pz = {}
+        py = {}
+
+        def rw_scalar(e):
+            g1[e] = rot.tile([P, 4 * H], BF16, name="g1", tag="g1", bufs=4, align_bytes=64)
+            dst, src = views(g1[e][:], w1raw[e][:])
+            nc.scalar.copy(out=dst[:, 0:SC_GROUPS], in_=src[:, 0:SC_GROUPS])
+
+        def rw_vector(e):
+            dst, src = views(g1[e][:], w1raw[e][:])
+            nc.vector.tensor_copy(out=dst[:, SC_GROUPS:128], in_=src[:, SC_GROUPS:128])
+
+        def qw(e):
+            w1c[e] = rot.tile([P, H], U32, name="w1c", tag="w1c", bufs=4, align_bytes=64)
+            w1s[e] = rot.tile([P, H], U8, name="w1s", tag="w1s", bufs=4, align_bytes=64)
+            nc.vector.quantize_mx(out=w1c[e][:].bitcast(FP8X4), scales=w1s[e][:], in_=g1[e][:])
+
+        def rw2(e):
+            g3[e] = rot.tile([P, 4 * L], BF16, name="g3", tag="g3", bufs=3, align_bytes=64)
+            dst, src = views(g3[e][:], w2raw[:, e * 512 : (e + 1) * 512])
+            nc.scalar.copy(out=dst, in_=src)
+
+        def qw2(e):
+            cols = slice(e * L, (e + 1) * L)
+            nc.vector.quantize_mx(out=w2c[:, cols].bitcast(FP8X4), scales=w2s[:, cols], in_=g3[e][:])
+
+        def mm1(e):
+            pz[e] = []
+            for t in range(4):
+                z = ps1.tile([P, 512], F32, name="z", tag="s1")
+                cols = slice(t * P, (t + 1) * P)
+                nc.tensor.matmul_mx(
+                    out=z[:],
+                    lhsT=w1c[e][:, cols].bitcast(FP8X4),
+                    lhsT_scale=w1s[e][:, cols],
+                    rhs=xc[:].bitcast(FP8X4),
+                    rhs_scale=xs[:],
+                    start=True,
+                    stop=True,
+                )
+                pz[e].append(z)
+
+        def tanh(e):
+            hT[e] = rot.tile([P, 4 * B], BF16, name="hT", tag="hT", bufs=3, align_bytes=64)
+            for t in range(4):
+                nc.scalar.activation(
+                    out=hT[e][:, t * B : (t + 1) * B],
+                    in_=pz[e][t][:],
+                    func=ACT.Tanh,
+                    bias=b1T[:, 4 * e + t : 4 * e + t + 1],
+                    scale=1.0,
+                )
+
+        def rh(e):
+            g2[e] = rot.tile([P, 4 * B], BF16, name="g2", tag="g2", bufs=3, align_bytes=64)
+            dst, src = views(g2[e][:], hT[e][:])
+            nc.vector.tensor_copy(out=dst, in_=src)
+
+        def qh(e):
+            hc[e] = rot.tile([P, B], U32, name="hc", tag="hc", bufs=3, align_bytes=64)
+            hs[e] = rot.tile([P, B], U8, name="hs", tag="hs", bufs=3, align_bytes=64)
+            nc.vector.quantize_mx(out=hc[e][:].bitcast(FP8X4), scales=hs[e][:], in_=g2[e][:])
+
+        def mm2(e):
+            py[e] = ps2.tile([P, 512], F32, name="y", tag="s2")
+            wcols = slice(e * L, (e + 1) * L)
+            for n in range(NB):
+                cols = slice(n * P, (n + 1) * P)
+                nc.tensor.matmul_mx(
+                    out=py[e][:, cols],
+                    lhsT=hc[e][:, cols].bitcast(FP8X4),
+                    lhsT_scale=hs[e][:, cols],
+                    rhs=w2c[:, wcols].bitcast(FP8X4),
+                    rhs_scale=w2s[:, wcols],
+                    start=True,
+                    stop=True,
+                )
+
+        def gb2(e):
+            for n in range(NB):
+                nc.vector.tensor_scalar(
+                    out=o3[:, n, e * L : (e + 1) * L],
+                    in0=b2b[:, e * L : (e + 1) * L],
+                    scalar1=g[:, n * E + e : n * E + e + 1],
+                    scalar2=None,
+                    op0=ALU.mult,
+                )
+
+        def fin(e):
+            for n in range(NB):
+                nc.vector.scalar_tensor_tensor(
+                    out=o3[:, n, e * L : (e + 1) * L],
+                    in0=py[e][:, n * P : (n + 1) * P],
+                    scalar=g[:, n * E + e : n * E + e + 1],
+                    in1=o3[:, n, e * L : (e + 1) * L],
+                    op0=ALU.mult,
+                    op1=ALU.add,
+                )
+
+        store_after = {3: 0, 7: 4, 11: 8, 13: 12, 14: 14, 15: 15}
+
+        def store(e):
+            if e in store_after:
+                cols = slice(store_after[e] * L, (e + 1) * L)
+                nc.sync.dma_start(out=out_v[:, :, cols], in_=o3[:, :, cols])
+
+        for e in range(3):
+            rw_scalar(e)
+            rw_vector(e)
+        rw2(0)
+        rw2(1)
+        qw(0)
+        qw(1)
+        qw2(0)
+        gb2(0)
+        mm1(0)
+        for i in range(E):
+            tanh(i)
+            if i + 1 < E:
+                mm1(i + 1)
+            if i + 3 < E:
+                rw_scalar(i + 3)
+            if i + 2 < E:
+                rw2(i + 2)
+            rh(i)
+            if i + 2 < E:
+                qw(i + 2)
+            qh(i)
+            mm2(i)
+            if i + 1 < E:
+                qw2(i + 1)
+            if i >= 1:
+                fin(i - 1)
+                store(i - 1)
+            if i + 3 < E:
+                rw_vector(i + 3)
+            if i + 1 < E:
+                gb2(i + 1)
+        fin(E - 1)
+        store(E - 1)

@@ -17,7 +17,15 @@ B, D, E, H, L = 512, 512, 16, 512, 128
 NB = B // P
 FLOPS = 2 * E * B * D * H + 2 * E * B * H * L
 
-SC_GROUPS = 56
+LOOKAHEAD = 4
+
+
+def scalar_groups(e):
+    if e == 0:
+        return 0
+    if e < LOOKAHEAD:
+        return 48
+    return 64
 
 
 def tile_mblfe_pa_kernel(tc, x, noise, clean_logits, noise_pre, W1, b1, W2, b2, out):
@@ -27,6 +35,7 @@ def tile_mblfe_pa_kernel(tc, x, noise, clean_logits, noise_pre, W1, b1, W2, b2, 
         rot = ctx.enter_context(tc.tile_pool(name="rot", bufs=3))
         ps1 = ctx.enter_context(tc.psum_pool(name="ps1", bufs=6))
         ps2 = ctx.enter_context(tc.psum_pool(name="ps2", bufs=2))
+        ctx.enter_context(tc.manual_schedule())
 
         x_sb = keep.tile([P, NB * D], BF16, name="x_sb", align_bytes=64)
         nc.sync.dma_start(out=x_sb[:], in_=x.rearrange("(p n) d -> p (n d)", n=NB))
@@ -55,48 +64,19 @@ def tile_mblfe_pa_kernel(tc, x, noise, clean_logits, noise_pre, W1, b1, W2, b2, 
         nc.vector.memset(b1raw[:], 0.0)
         nc.scalar.dma_start(out=b1raw[0:64, :], in_=b1.rearrange("e (t p) -> (e t) p", p=P))
 
-        load_w1(0)
-        load_w1(1)
-        load_w2(0)
-        load_w1(2)
-        load_w1(3)
-        nc.sync.dma_start(out=b2b[:], in_=b2.rearrange("e l -> (e l)").partition_broadcast(P))
-        for e in range(4, E):
+        for e in range(3):
             load_w1(e)
-            if e % 4 == 0:
-                load_w2(e // 4)
+        load_w2(0)
+        load_w1(3)
+        load_w1(4)
+        nc.sync.dma_start(out=b2b[:], in_=b2.rearrange("e l -> (e l)").partition_broadcast(P))
+        for e in range(5, E):
+            load_w1(e)
+            if e in (6, 8, 10):
+                load_w2((e - 4) // 2)
 
         ident = keep.tile([P, P], F32, name="ident")
         make_identity(nc, ident[:])
-
-        x32 = x_sb[:].bitcast(F32).rearrange("p (n q u) -> p n u q", n=NB, u=2)
-        gx = keep.tile([P, 4 * B], BF16, name="gx", align_bytes=64)
-        gx32 = gx[:].bitcast(F32)
-        xc = keep.tile([P, B], U32, name="xc", align_bytes=64)
-        xs = keep.tile([P, B], U8, name="xs", align_bytes=64)
-        for half in range(2):
-            xt = ps1.tile([P, 512], F32, name="xt", tag="s1")
-            for m in range(2):
-                for u in range(2):
-                    nc.tensor.transpose(
-                        out=xt[:, (2 * m + u) * P : (2 * m + u + 1) * P],
-                        in_=x32[:, 2 * half + m, u, :],
-                        identity=ident[:],
-                    )
-            dst = gx32[:, half * 512 : (half + 1) * 512].rearrange("p (m b u) -> p m b u", m=2, u=2)
-            src = xt[:].rearrange("p (m u b) -> p m b u", m=2, u=2)
-            if half == 0:
-                nc.vector.tensor_copy(out=dst, in_=src)
-            else:
-                nc.scalar.copy(out=dst, in_=src)
-        nc.vector.quantize_mx(out=xc[:].bitcast(FP8X4), scales=xs[:], in_=gx[:])
-
-        b1f = keep.tile([P, P], F32, name="b1f")
-        nc.vector.tensor_copy(out=b1f[:], in_=b1raw[:])
-        pb = ps2.tile([P, 512], F32, name="pb", tag="s2")
-        nc.tensor.transpose(out=pb[:, 0:P], in_=b1f[:], identity=ident[:])
-        b1T = keep.tile([P, 4 * E], F32, name="b1T")
-        nc.vector.tensor_copy(out=b1T[:], in_=pb[:, 0 : 4 * E])
 
         def gt(name, w=NB * E):
             return keep.tile([P, w], F32, name=name)
@@ -108,43 +88,51 @@ def tile_mblfe_pa_kernel(tc, x, noise, clean_logits, noise_pre, W1, b1, W2, b2, 
             return t[:].unsqueeze(2).to_broadcast([P, NB, E])
 
         nabs = gt("nabs")
-        nc.vector.scalar_tensor_tensor(out=nabs[:], in0=np_in[:], scalar=-1.0, in1=np_in[:], op0=ALU.mult, op1=ALU.min)
         eu = gt("eu")
-        nc.scalar.activation(out=eu[:], in_=nabs[:], func=ACT.Exp)
         lg = gt("lg")
-        nc.scalar.activation(out=lg[:], in_=eu[:], func=ACT.Ln, bias=1.0, scale=1.0)
         sp = gt("sp")
-        nc.vector.scalar_tensor_tensor(out=sp[:], in0=np_in[:], scalar=0.0, in1=lg[:], op0=ALU.max, op1=ALU.add)
         nz = gt("nz")
-        nc.vector.scalar_tensor_tensor(out=nz[:], in0=sp[:], scalar=0.01, in1=no_in[:], op0=ALU.add, op1=ALU.mult)
         lo = gt("lo")
-        nc.vector.tensor_tensor(out=lo[:], in0=nz[:], in1=cl_in[:], op=ALU.add)
         mx = gt("mx", NB)
-        nc.vector.tensor_reduce(out=mx[:], in_=v3(lo), axis=AX.X, op=ALU.max)
         ls = gt("ls")
-        nc.vector.tensor_tensor(out=v3(ls), in0=v3(lo), in1=bc(mx), op=ALU.subtract)
         ex = gt("ex")
-        nc.scalar.activation(out=ex[:], in_=ls[:], func=ACT.Exp)
         sm = gt("sm", NB)
-        nc.vector.tensor_reduce(out=sm[:], in_=v3(ex), axis=AX.X, op=ALU.add)
         rs = gt("rs", NB)
-        nc.vector.reciprocal(out=rs[:], in_=sm[:])
         pr = gt("pr")
-        nc.vector.tensor_tensor(out=v3(pr), in0=v3(ex), in1=bc(rs), op=ALU.mult)
         pm = gt("pm", NB)
-        nc.vector.tensor_reduce(out=pm[:], in_=v3(pr), axis=AX.X, op=ALU.add)
         th = gt("th", NB)
-        nc.vector.tensor_scalar(out=th[:], in0=pm[:], scalar1=1.0 / E, scalar2=-1e-8, op0=ALU.mult, op1=ALU.add)
         mk = gt("mk")
-        nc.vector.tensor_tensor(out=v3(mk), in0=v3(pr), in1=bc(th), op=ALU.is_ge)
         gq = gt("gq")
-        nc.vector.tensor_tensor(out=gq[:], in0=pr[:], in1=mk[:], op=ALU.mult)
         gs = gt("gs", NB)
-        nc.vector.tensor_reduce(out=gs[:], in_=v3(gq), axis=AX.X, op=ALU.add)
         rg = gt("rg", NB)
-        nc.vector.reciprocal(out=rg[:], in_=gs[:])
         g = gt("g")
-        nc.vector.tensor_tensor(out=v3(g), in0=v3(gq), in1=bc(rg), op=ALU.mult)
+
+        gate_steps = [
+            lambda: nc.vector.scalar_tensor_tensor(out=sp[:], in0=np_in[:], scalar=0.0, in1=lg[:], op0=ALU.max, op1=ALU.add),
+            lambda: nc.vector.scalar_tensor_tensor(out=nz[:], in0=sp[:], scalar=0.01, in1=no_in[:], op0=ALU.add, op1=ALU.mult),
+            lambda: nc.vector.tensor_tensor(out=lo[:], in0=nz[:], in1=cl_in[:], op=ALU.add),
+            lambda: nc.vector.tensor_reduce(out=mx[:], in_=v3(lo), axis=AX.X, op=ALU.max),
+            lambda: nc.vector.tensor_tensor(out=v3(ls), in0=v3(lo), in1=bc(mx), op=ALU.subtract),
+            lambda: nc.vector.tensor_reduce(out=sm[:], in_=v3(ex), axis=AX.X, op=ALU.add),
+            lambda: nc.vector.reciprocal(out=rs[:], in_=sm[:]),
+            lambda: nc.vector.tensor_tensor(out=v3(pr), in0=v3(ex), in1=bc(rs), op=ALU.mult),
+            lambda: nc.vector.tensor_reduce(out=pm[:], in_=v3(pr), axis=AX.X, op=ALU.add),
+            lambda: nc.vector.tensor_scalar(out=th[:], in0=pm[:], scalar1=1.0 / E, scalar2=-1e-8, op0=ALU.mult, op1=ALU.add),
+            lambda: nc.vector.tensor_tensor(out=v3(mk), in0=v3(pr), in1=bc(th), op=ALU.is_ge),
+            lambda: nc.vector.tensor_tensor(out=gq[:], in0=pr[:], in1=mk[:], op=ALU.mult),
+            lambda: nc.vector.tensor_reduce(out=gs[:], in_=v3(gq), axis=AX.X, op=ALU.add),
+            lambda: nc.vector.reciprocal(out=rg[:], in_=gs[:]),
+            lambda: nc.vector.tensor_tensor(out=v3(g), in0=v3(gq), in1=bc(rg), op=ALU.mult),
+        ]
+        taken = [0]
+
+        def gate(count=1):
+            for k in range(count):
+                if taken[0] < len(gate_steps):
+                    gate_steps[taken[0]]()
+                    taken[0] = taken[0] + 1
+                    if taken[0] == 5:
+                        nc.scalar.activation(out=ex[:], in_=ls[:], func=ACT.Exp)
 
         o = keep.tile([P, NB * E * L], F32, name="o")
         o3 = o[:].rearrange("p (n c) -> p n c", n=NB)
@@ -170,20 +158,23 @@ def tile_mblfe_pa_kernel(tc, x, noise, clean_logits, noise_pre, W1, b1, W2, b2, 
 
         def rw_scalar(e):
             g1[e] = rot.tile([P, 4 * H], BF16, name="g1", tag="g1", bufs=4, align_bytes=64)
-            dst, src = views(g1[e][:], w1raw[e][:])
-            nc.scalar.copy(out=dst[:, 0:SC_GROUPS], in_=src[:, 0:SC_GROUPS])
+            k = scalar_groups(e)
+            if k > 0:
+                dst, src = views(g1[e][:], w1raw[e][:])
+                nc.scalar.copy(out=dst[:, 0:k], in_=src[:, 0:k])
 
         def rw_vector(e):
+            k = scalar_groups(e)
             dst, src = views(g1[e][:], w1raw[e][:])
-            nc.vector.tensor_copy(out=dst[:, SC_GROUPS:128], in_=src[:, SC_GROUPS:128])
+            nc.vector.tensor_copy(out=dst[:, k:128], in_=src[:, k:128])
 
         def qw(e):
-            w1c[e] = rot.tile([P, H], U32, name="w1c", tag="w1c", bufs=4, align_bytes=64)
-            w1s[e] = rot.tile([P, H], U8, name="w1s", tag="w1s", bufs=4, align_bytes=64)
+            w1c[e] = rot.tile([P, H], U32, name="w1c", tag="w1c", bufs=5, align_bytes=64)
+            w1s[e] = rot.tile([P, H], U8, name="w1s", tag="w1s", bufs=5, align_bytes=64)
             nc.vector.quantize_mx(out=w1c[e][:].bitcast(FP8X4), scales=w1s[e][:], in_=g1[e][:])
 
         def rw2(e):
-            g3[e] = rot.tile([P, 4 * L], BF16, name="g3", tag="g3", bufs=3, align_bytes=64)
+            g3[e] = rot.tile([P, 4 * L], BF16, name="g3", tag="g3", bufs=5, align_bytes=64)
             dst, src = views(g3[e][:], w2raw[:, e * 512 : (e + 1) * 512])
             nc.scalar.copy(out=dst, in_=src)
 
@@ -253,6 +244,8 @@ def tile_mblfe_pa_kernel(tc, x, noise, clean_logits, noise_pre, W1, b1, W2, b2, 
                     op0=ALU.mult,
                 )
 
+        store_after = {3: 0, 7: 4, 11: 8, 13: 12, 14: 14, 15: 15}
+
         def fin(e):
             for n in range(NB):
                 nc.vector.scalar_tensor_tensor(
@@ -263,45 +256,86 @@ def tile_mblfe_pa_kernel(tc, x, noise, clean_logits, noise_pre, W1, b1, W2, b2, 
                     op0=ALU.mult,
                     op1=ALU.add,
                 )
-
-        store_after = {3: 0, 7: 4, 11: 8, 13: 12, 14: 14, 15: 15}
-
-        def store(e):
             if e in store_after:
                 cols = slice(store_after[e] * L, (e + 1) * L)
                 nc.sync.dma_start(out=out_v[:, :, cols], in_=o3[:, :, cols])
 
-        for e in range(3):
+        nc.vector.scalar_tensor_tensor(out=nabs[:], in0=np_in[:], scalar=-1.0, in1=np_in[:], op0=ALU.mult, op1=ALU.min)
+        nc.scalar.activation(out=eu[:], in_=nabs[:], func=ACT.Exp)
+        nc.scalar.activation(out=lg[:], in_=eu[:], func=ACT.Ln, bias=1.0, scale=1.0)
+
+        x32 = x_sb[:].bitcast(F32).rearrange("p (n q u) -> p n u q", n=NB, u=2)
+        gx = keep.tile([P, 4 * B], BF16, name="gx", align_bytes=64)
+        gx32 = gx[:].bitcast(F32)
+        xc = keep.tile([P, B], U32, name="xc", align_bytes=64)
+        xs = keep.tile([P, B], U8, name="xs", align_bytes=64)
+        xt = []
+        for half in range(2):
+            xt.append(ps1.tile([P, 512], F32, name="xt", tag="s1"))
+            for m in range(2):
+                for u in range(2):
+                    nc.tensor.transpose(
+                        out=xt[half][:, (2 * m + u) * P : (2 * m + u + 1) * P],
+                        in_=x32[:, 2 * half + m, u, :],
+                        identity=ident[:],
+                    )
+        b1f = keep.tile([P, P], F32, name="b1f")
+        nc.vector.tensor_copy(out=b1f[:], in_=b1raw[:])
+        pb = ps2.tile([P, 512], F32, name="pb", tag="s2")
+        nc.tensor.transpose(out=pb[:, 0:P], in_=b1f[:], identity=ident[:])
+        for half in range(2):
+            dst = gx32[:, half * 512 : (half + 1) * 512].rearrange("p (m b u) -> p m b u", m=2, u=2)
+            src = xt[half][:].rearrange("p (m u b) -> p m b u", m=2, u=2)
+            if half == 0:
+                nc.vector.tensor_copy(out=dst, in_=src)
+            else:
+                nc.scalar.copy(out=dst, in_=src)
+
+        rw_scalar(0)
+        rw_vector(0)
+        gate()
+        qw(0)
+        gate()
+        nc.vector.quantize_mx(out=xc[:].bitcast(FP8X4), scales=xs[:], in_=gx[:])
+        b1T = keep.tile([P, 4 * E], F32, name="b1T")
+        nc.vector.tensor_copy(out=b1T[:], in_=pb[:, 0 : 4 * E])
+        mm1(0)
+        for e in range(1, LOOKAHEAD):
             rw_scalar(e)
             rw_vector(e)
-        rw2(0)
-        rw2(1)
-        qw(0)
-        qw(1)
-        qw2(0)
-        gb2(0)
-        mm1(0)
+            gate()
+            if e >= 2:
+                qw(e - 1)
+            gate()
+        for e in range(LOOKAHEAD):
+            rw2(e)
+        gate()
+        for e in range(LOOKAHEAD):
+            qw2(e)
+            gate()
+        gate(len(gate_steps))
+        for e in range(LOOKAHEAD):
+            gb2(e)
+
         for i in range(E):
+            a = i + LOOKAHEAD
             tanh(i)
+            if a < E:
+                rw_scalar(a)
+                rw2(a)
             if i + 1 < E:
                 mm1(i + 1)
-            if i + 3 < E:
-                rw_scalar(i + 3)
-            if i + 2 < E:
-                rw2(i + 2)
+            if i >= 1:
+                mm2(i - 1)
             rh(i)
-            if i + 2 < E:
-                qw(i + 2)
-            qh(i)
-            mm2(i)
-            if i + 1 < E:
-                qw2(i + 1)
             if i >= 1:
                 fin(i - 1)
-                store(i - 1)
-            if i + 3 < E:
-                rw_vector(i + 3)
-            if i + 1 < E:
-                gb2(i + 1)
+            if a - 1 < E:
+                qw(a - 1)
+            qh(i)
+            if a < E:
+                rw_vector(a)
+                gb2(a)
+                qw2(a)
+        mm2(E - 1)
         fin(E - 1)
-        store(E - 1)

@@ -17,15 +17,11 @@ B, D, E, H, L = 512, 512, 16, 512, 128
 NB = B // P
 FLOPS = 2 * E * B * D * H + 2 * E * B * H * L
 
-LOOKAHEAD = 4
+FIRST_VECTOR_GATING = 12
 
 
 def scalar_groups(e):
-    if e == 0:
-        return 0
-    if e < LOOKAHEAD:
-        return 48
-    return 64
+    return (32, 0, 0)[e] if e < 3 else 16
 
 
 def tile_mblfe_pa_kernel(tc, x, noise, clean_logits, noise_pre, W1, b1, W2, b2, out):
@@ -33,7 +29,8 @@ def tile_mblfe_pa_kernel(tc, x, noise, clean_logits, noise_pre, W1, b1, W2, b2, 
     with ExitStack() as ctx:
         keep = ctx.enter_context(tc.tile_pool(name="keep", bufs=1))
         rot = ctx.enter_context(tc.tile_pool(name="rot", bufs=3))
-        ps1 = ctx.enter_context(tc.psum_pool(name="ps1", bufs=6))
+        ps1 = ctx.enter_context(tc.psum_pool(name="ps1", bufs=5))
+        psy = ctx.enter_context(tc.psum_pool(name="psy", bufs=1))
         ps2 = ctx.enter_context(tc.psum_pool(name="ps2", bufs=2))
         ctx.enter_context(tc.manual_schedule())
 
@@ -43,7 +40,6 @@ def tile_mblfe_pa_kernel(tc, x, noise, clean_logits, noise_pre, W1, b1, W2, b2, 
         for e in range(E):
             w1raw.append(keep.tile([P, 4 * H], BF16, name="w1raw%d" % e, align_bytes=64))
         w2raw = keep.tile([P, E * 4 * L], BF16, name="w2raw", align_bytes=64)
-        b2b = keep.tile([P, E * L], BF16, name="b2b", align_bytes=64)
 
         def load_w1(e):
             nc.sync.dma_start(out=w1raw[e][:], in_=W1[e].rearrange("(p j) h -> p (j h)", j=4))
@@ -63,17 +59,15 @@ def tile_mblfe_pa_kernel(tc, x, noise, clean_logits, noise_pre, W1, b1, W2, b2, 
         b1raw = keep.tile([P, P], BF16, name="b1raw")
         nc.vector.memset(b1raw[:], 0.0)
         nc.scalar.dma_start(out=b1raw[0:64, :], in_=b1.rearrange("e (t p) -> (e t) p", p=P))
+        nc.scalar.dma_start(out=b1raw[64:80, :], in_=b2)
 
-        for e in range(3):
-            load_w1(e)
+        load_w1(0)
+        load_w1(1)
         load_w2(0)
-        load_w1(3)
-        load_w1(4)
-        nc.sync.dma_start(out=b2b[:], in_=b2.rearrange("e l -> (e l)").partition_broadcast(P))
-        for e in range(5, E):
+        for e in range(2, E):
             load_w1(e)
-            if e in (6, 8, 10):
-                load_w2((e - 4) // 2)
+            if e in (5, 9, 12):
+                load_w2((e + 1) // 4)
 
         ident = keep.tile([P, P], F32, name="ident")
         make_identity(nc, ident[:])
@@ -155,6 +149,8 @@ def tile_mblfe_pa_kernel(tc, x, noise, clean_logits, noise_pre, W1, b1, W2, b2, 
         hs = {}
         pz = {}
         py = {}
+        ys = {}
+        pt = {}
 
         def rw_scalar(e):
             g1[e] = rot.tile([P, 4 * H], BF16, name="g1", tag="g1", bufs=4, align_bytes=64)
@@ -176,7 +172,7 @@ def tile_mblfe_pa_kernel(tc, x, noise, clean_logits, noise_pre, W1, b1, W2, b2, 
         def rw2(e):
             g3[e] = rot.tile([P, 4 * L], BF16, name="g3", tag="g3", bufs=5, align_bytes=64)
             dst, src = views(g3[e][:], w2raw[:, e * 512 : (e + 1) * 512])
-            nc.scalar.copy(out=dst, in_=src)
+            nc.vector.tensor_copy(out=dst, in_=src)
 
         def qw2(e):
             cols = slice(e * L, (e + 1) * L)
@@ -220,42 +216,50 @@ def tile_mblfe_pa_kernel(tc, x, noise, clean_logits, noise_pre, W1, b1, W2, b2, 
             nc.vector.quantize_mx(out=hc[e][:].bitcast(FP8X4), scales=hs[e][:], in_=g2[e][:])
 
         def mm2(e):
-            py[e] = ps2.tile([P, 512], F32, name="y", tag="s2")
+            py[e] = psy.tile([P, 512], F32, name="y", tag="y")
             wcols = slice(e * L, (e + 1) * L)
+            nc.tensor.matmul_mx(
+                out=py[e][:],
+                lhsT=w2c[:, wcols].bitcast(FP8X4),
+                lhsT_scale=w2s[:, wcols],
+                rhs=hc[e][:].bitcast(FP8X4),
+                rhs_scale=hs[e][:],
+                start=True,
+                stop=True,
+            )
+
+        def yb(e):
+            ys[e] = rot.tile([P, B], F32, name="ys", tag="ys", bufs=2)
+            nc.scalar.activation(
+                out=ys[e][:], in_=py[e][:], func=ACT.Identity, bias=b1T[:, 4 * E + e : 4 * E + e + 1], scale=1.0
+            )
+
+        def tr(e):
+            pt[e] = ps2.tile([P, 512], F32, name="pt", tag="s2")
             for n in range(NB):
                 cols = slice(n * P, (n + 1) * P)
-                nc.tensor.matmul_mx(
-                    out=py[e][:, cols],
-                    lhsT=hc[e][:, cols].bitcast(FP8X4),
-                    lhsT_scale=hs[e][:, cols],
-                    rhs=w2c[:, wcols].bitcast(FP8X4),
-                    rhs_scale=w2s[:, wcols],
-                    start=True,
-                    stop=True,
-                )
-
-        def gb2(e):
-            for n in range(NB):
-                nc.vector.tensor_scalar(
-                    out=o3[:, n, e * L : (e + 1) * L],
-                    in0=b2b[:, e * L : (e + 1) * L],
-                    scalar1=g[:, n * E + e : n * E + e + 1],
-                    scalar2=None,
-                    op0=ALU.mult,
-                )
+                nc.tensor.transpose(out=pt[e][:, cols], in_=ys[e][:, cols], identity=ident[:])
 
         store_after = {3: 0, 7: 4, 11: 8, 13: 12, 14: 14, 15: 15}
+        g3d = g[:].rearrange("p (n e) -> p n e", n=NB)
 
-        def fin(e):
-            for n in range(NB):
-                nc.vector.scalar_tensor_tensor(
-                    out=o3[:, n, e * L : (e + 1) * L],
-                    in0=py[e][:, n * P : (n + 1) * P],
-                    scalar=g[:, n * E + e : n * E + e + 1],
-                    in1=o3[:, n, e * L : (e + 1) * L],
-                    op0=ALU.mult,
-                    op1=ALU.add,
+        def mul(e):
+            ecols = slice(e * L, (e + 1) * L)
+            if e >= FIRST_VECTOR_GATING:
+                nc.vector.tensor_tensor(
+                    out=o3[:, :, ecols],
+                    in0=pt[e][:].rearrange("p (n l) -> p n l", n=NB),
+                    in1=g3d[:, :, e : e + 1].to_broadcast([P, NB, L]),
+                    op=ALU.mult,
                 )
+            else:
+                for n in range(NB):
+                    nc.scalar.activation(
+                        out=o3[:, n, ecols],
+                        in_=pt[e][:, n * P : (n + 1) * P],
+                        func=ACT.Copy,
+                        scale=g[:, n * E + e : n * E + e + 1],
+                    )
             if e in store_after:
                 cols = slice(store_after[e] * L, (e + 1) * L)
                 nc.sync.dma_start(out=out_v[:, :, cols], in_=o3[:, :, cols])
@@ -293,49 +297,58 @@ def tile_mblfe_pa_kernel(tc, x, noise, clean_logits, noise_pre, W1, b1, W2, b2, 
 
         rw_scalar(0)
         rw_vector(0)
-        gate()
-        qw(0)
-        gate()
+        gate(2)
         nc.vector.quantize_mx(out=xc[:].bitcast(FP8X4), scales=xs[:], in_=gx[:])
-        b1T = keep.tile([P, 4 * E], F32, name="b1T")
-        nc.vector.tensor_copy(out=b1T[:], in_=pb[:, 0 : 4 * E])
-        mm1(0)
-        for e in range(1, LOOKAHEAD):
-            rw_scalar(e)
-            rw_vector(e)
-            gate()
-            if e >= 2:
-                qw(e - 1)
-            gate()
-        for e in range(LOOKAHEAD):
-            rw2(e)
         gate()
-        for e in range(LOOKAHEAD):
-            qw2(e)
-            gate()
-        gate(len(gate_steps))
-        for e in range(LOOKAHEAD):
-            gb2(e)
+        b1T = keep.tile([P, 5 * E], F32, name="b1T")
+        nc.vector.tensor_copy(out=b1T[:], in_=pb[:, 0 : 5 * E])
+        qw(0)
+        gate(2)
+        mm1(0)
+        rw_scalar(1)
+        rw_vector(1)
+        rw2(0)
+        gate()
+        qw(1)
+        gate()
+        rw_scalar(2)
+        rw_vector(2)
+        gate()
+        qw2(0)
+        gate()
 
         for i in range(E):
-            a = i + LOOKAHEAD
             tanh(i)
-            if a < E:
-                rw_scalar(a)
-                rw2(a)
+            if i >= 2 and i - 2 < FIRST_VECTOR_GATING:
+                mul(i - 2)
+            if i + 3 < E:
+                rw_scalar(i + 3)
+            if i >= 1:
+                yb(i - 1)
             if i + 1 < E:
                 mm1(i + 1)
             if i >= 1:
-                mm2(i - 1)
+                tr(i - 1)
             rh(i)
-            if i >= 1:
-                fin(i - 1)
-            if a - 1 < E:
-                qw(a - 1)
+            gate()
+            if i + 2 < E:
+                qw(i + 2)
+            gate()
+            if i >= 2 and i - 2 >= FIRST_VECTOR_GATING:
+                mul(i - 2)
             qh(i)
-            if a < E:
-                rw_vector(a)
-                gb2(a)
-                qw2(a)
-        mm2(E - 1)
-        fin(E - 1)
+            gate()
+            mm2(i)
+            if i + 1 < E:
+                rw2(i + 1)
+            gate()
+            if i + 3 < E:
+                rw_vector(i + 3)
+            gate()
+            if i + 1 < E:
+                qw2(i + 1)
+            gate()
+        yb(E - 1)
+        mul(E - 2)
+        tr(E - 1)
+        mul(E - 1)

@@ -21,7 +21,7 @@ FIRST_VECTOR_GATING = 12
 
 
 def scalar_groups(e):
-    return (32, 0, 0)[e] if e < 3 else 16
+    return 0 if e < 3 else 8
 
 
 def tile_mblfe_pa_kernel(tc, x, noise, clean_logits, noise_pre, W1, b1, W2, b2, out):
@@ -35,10 +35,20 @@ def tile_mblfe_pa_kernel(tc, x, noise, clean_logits, noise_pre, W1, b1, W2, b2, 
         ctx.enter_context(tc.manual_schedule())
 
         x_sb = keep.tile([P, NB * D], BF16, name="x_sb", align_bytes=64)
-        nc.sync.dma_start(out=x_sb[:], in_=x.rearrange("(p n) d -> p (n d)", n=NB))
         w1raw = []
         for e in range(E):
             w1raw.append(keep.tile([P, 4 * H], BF16, name="w1raw%d" % e, align_bytes=64))
+
+        def load_w1_half(e, k):
+            cols = slice(k * (H // 2), (k + 1) * (H // 2))
+            nc.sync.dma_start(
+                out=w1raw[e][:].rearrange("p (j h) -> p j h", j=4)[:, :, cols],
+                in_=W1[e].rearrange("(p j) h -> p j h", j=4)[:, :, cols],
+            )
+
+        load_w1_half(0, 0)
+        nc.sync.dma_start(out=x_sb[:], in_=x.rearrange("(p n) d -> p (n d)", n=NB))
+        load_w1_half(0, 1)
         w2raw = keep.tile([P, E * 4 * L], BF16, name="w2raw", align_bytes=64)
 
         def load_w1(e):
@@ -60,8 +70,9 @@ def tile_mblfe_pa_kernel(tc, x, noise, clean_logits, noise_pre, W1, b1, W2, b2, 
         nc.vector.memset(b1raw[:], 0.0)
         nc.scalar.dma_start(out=b1raw[0:64, :], in_=b1.rearrange("e (t p) -> (e t) p", p=P))
         nc.scalar.dma_start(out=b1raw[64:80, :], in_=b2)
+        b2last = keep.tile([P, L], BF16, name="b2last")
+        nc.scalar.dma_start(out=b2last[:], in_=b2[E - 1].partition_broadcast(P))
 
-        load_w1(0)
         load_w1(1)
         load_w2(0)
         for e in range(2, E):
@@ -93,9 +104,6 @@ def tile_mblfe_pa_kernel(tc, x, noise, clean_logits, noise_pre, W1, b1, W2, b2, 
         sm = gt("sm", NB)
         rs = gt("rs", NB)
         pr = gt("pr")
-        pm = gt("pm", NB)
-        th = gt("th", NB)
-        mk = gt("mk")
         gq = gt("gq")
         gs = gt("gs", NB)
         rg = gt("rg", NB)
@@ -110,10 +118,7 @@ def tile_mblfe_pa_kernel(tc, x, noise, clean_logits, noise_pre, W1, b1, W2, b2, 
             lambda: nc.vector.tensor_reduce(out=sm[:], in_=v3(ex), axis=AX.X, op=ALU.add),
             lambda: nc.vector.reciprocal(out=rs[:], in_=sm[:]),
             lambda: nc.vector.tensor_tensor(out=v3(pr), in0=v3(ex), in1=bc(rs), op=ALU.mult),
-            lambda: nc.vector.tensor_reduce(out=pm[:], in_=v3(pr), axis=AX.X, op=ALU.add),
-            lambda: nc.vector.tensor_scalar(out=th[:], in0=pm[:], scalar1=1.0 / E, scalar2=-1e-8, op0=ALU.mult, op1=ALU.add),
-            lambda: nc.vector.tensor_tensor(out=v3(mk), in0=v3(pr), in1=bc(th), op=ALU.is_ge),
-            lambda: nc.vector.tensor_tensor(out=gq[:], in0=pr[:], in1=mk[:], op=ALU.mult),
+            lambda: nc.vector.scalar_tensor_tensor(out=gq[:], in0=pr[:], scalar=1.0 / E - 1e-8, in1=pr[:], op0=ALU.is_ge, op1=ALU.mult),
             lambda: nc.vector.tensor_reduce(out=gs[:], in_=v3(gq), axis=AX.X, op=ALU.add),
             lambda: nc.vector.reciprocal(out=rg[:], in_=gs[:]),
             lambda: nc.vector.tensor_tensor(out=v3(g), in0=v3(gq), in1=bc(rg), op=ALU.mult),
@@ -159,10 +164,10 @@ def tile_mblfe_pa_kernel(tc, x, noise, clean_logits, noise_pre, W1, b1, W2, b2, 
                 dst, src = views(g1[e][:], w1raw[e][:])
                 nc.scalar.copy(out=dst[:, 0:k], in_=src[:, 0:k])
 
-        def rw_vector(e):
-            k = scalar_groups(e)
+        def rw_vector(e, lo_group=None, hi_group=128):
+            k = scalar_groups(e) if lo_group is None else lo_group
             dst, src = views(g1[e][:], w1raw[e][:])
-            nc.vector.tensor_copy(out=dst[:, k:128], in_=src[:, k:128])
+            nc.vector.tensor_copy(out=dst[:, k:hi_group], in_=src[:, k:hi_group])
 
         def qw(e):
             w1c[e] = rot.tile([P, H], U32, name="w1c", tag="w1c", bufs=5, align_bytes=64)
@@ -240,7 +245,7 @@ def tile_mblfe_pa_kernel(tc, x, noise, clean_logits, noise_pre, W1, b1, W2, b2, 
                 cols = slice(n * P, (n + 1) * P)
                 nc.tensor.transpose(out=pt[e][:, cols], in_=ys[e][:, cols], identity=ident[:])
 
-        store_after = {3: 0, 7: 4, 11: 8, 13: 12, 14: 14, 15: 15}
+        store_after = {3: 0, 7: 4, 11: 8, 13: 12, 14: 14}
         g3d = g[:].rearrange("p (n e) -> p n e", n=NB)
 
         def mul(e):
@@ -264,6 +269,87 @@ def tile_mblfe_pa_kernel(tc, x, noise, clean_logits, noise_pre, W1, b1, W2, b2, 
                 cols = slice(store_after[e] * L, (e + 1) * L)
                 nc.sync.dma_start(out=out_v[:, :, cols], in_=o3[:, :, cols])
 
+        LAST = E - 1
+        lcols = slice(LAST * L, (LAST + 1) * L)
+        HB = B // 2
+
+        def gb2_last():
+            for n in range(NB):
+                nc.vector.tensor_scalar(
+                    out=o3[:, n, lcols],
+                    in0=b2last[:],
+                    scalar1=g[:, n * E + LAST : n * E + LAST + 1],
+                    scalar2=None,
+                    op0=ALU.mult,
+                )
+
+        def mm1_last(h):
+            pz[(LAST, h)] = []
+            for t in range(4):
+                z = ps1.tile([P, 512], F32, name="z", tag="s1")
+                cols = slice(t * P, (t + 1) * P)
+                bcols = slice(h * HB, (h + 1) * HB)
+                nc.tensor.matmul_mx(
+                    out=z[:, 0:HB],
+                    lhsT=w1c[LAST][:, cols].bitcast(FP8X4),
+                    lhsT_scale=w1s[LAST][:, cols],
+                    rhs=xc[:, bcols].bitcast(FP8X4),
+                    rhs_scale=xs[:, bcols],
+                    start=True,
+                    stop=True,
+                )
+                pz[(LAST, h)].append(z)
+
+        def tanh_last(h):
+            hT[(LAST, h)] = rot.tile([P, 4 * HB], BF16, name="hT", tag="hT", bufs=3, align_bytes=64)
+            for t in range(4):
+                nc.scalar.activation(
+                    out=hT[(LAST, h)][:, t * HB : (t + 1) * HB],
+                    in_=pz[(LAST, h)][t][:, 0:HB],
+                    func=ACT.Tanh,
+                    bias=b1T[:, 4 * LAST + t : 4 * LAST + t + 1],
+                    scale=1.0,
+                )
+
+        def rh_last(h):
+            g2[(LAST, h)] = rot.tile([P, 4 * HB], BF16, name="g2", tag="g2", bufs=3, align_bytes=64)
+            dst, src = views(g2[(LAST, h)][:], hT[(LAST, h)][:])
+            nc.vector.tensor_copy(out=dst, in_=src)
+
+        def qh_last(h):
+            hc[(LAST, h)] = rot.tile([P, HB], U32, name="hc", tag="hc", bufs=3, align_bytes=64)
+            hs[(LAST, h)] = rot.tile([P, HB], U8, name="hs", tag="hs", bufs=3, align_bytes=64)
+            nc.vector.quantize_mx(
+                out=hc[(LAST, h)][:].bitcast(FP8X4), scales=hs[(LAST, h)][:], in_=g2[(LAST, h)][:]
+            )
+
+        def mm2_last(h):
+            py[(LAST, h)] = ps2.tile([P, 512], F32, name="yl", tag="s2")
+            for m in range(2):
+                cols = slice(m * P, (m + 1) * P)
+                nc.tensor.matmul_mx(
+                    out=py[(LAST, h)][:, cols],
+                    lhsT=hc[(LAST, h)][:, cols].bitcast(FP8X4),
+                    lhsT_scale=hs[(LAST, h)][:, cols],
+                    rhs=w2c[:, lcols].bitcast(FP8X4),
+                    rhs_scale=w2s[:, lcols],
+                    start=True,
+                    stop=True,
+                )
+
+        def fin_last(h):
+            for m in range(2):
+                n = 2 * h + m
+                nc.vector.scalar_tensor_tensor(
+                    out=o3[:, n, lcols],
+                    in0=py[(LAST, h)][:, m * P : (m + 1) * P],
+                    scalar=g[:, n * E + LAST : n * E + LAST + 1],
+                    in1=o3[:, n, lcols],
+                    op0=ALU.mult,
+                    op1=ALU.add,
+                )
+            nc.sync.dma_start(out=out_v[:, 2 * h : 2 * h + 2, lcols], in_=o3[:, 2 * h : 2 * h + 2, lcols])
+
         nc.vector.scalar_tensor_tensor(out=nabs[:], in0=np_in[:], scalar=-1.0, in1=np_in[:], op0=ALU.mult, op1=ALU.min)
         nc.scalar.activation(out=eu[:], in_=nabs[:], func=ACT.Exp)
         nc.scalar.activation(out=lg[:], in_=eu[:], func=ACT.Ln, bias=1.0, scale=1.0)
@@ -283,6 +369,8 @@ def tile_mblfe_pa_kernel(tc, x, noise, clean_logits, noise_pre, W1, b1, W2, b2, 
                         in_=x32[:, 2 * half + m, u, :],
                         identity=ident[:],
                     )
+        rw_scalar(0)
+        rw_vector(0, 0, 64)
         b1f = keep.tile([P, P], F32, name="b1f")
         nc.vector.tensor_copy(out=b1f[:], in_=b1raw[:])
         pb = ps2.tile([P, 512], F32, name="pb", tag="s2")
@@ -290,25 +378,21 @@ def tile_mblfe_pa_kernel(tc, x, noise, clean_logits, noise_pre, W1, b1, W2, b2, 
         for half in range(2):
             dst = gx32[:, half * 512 : (half + 1) * 512].rearrange("p (m b u) -> p m b u", m=2, u=2)
             src = xt[half][:].rearrange("p (m u b) -> p m b u", m=2, u=2)
-            if half == 0:
-                nc.vector.tensor_copy(out=dst, in_=src)
-            else:
-                nc.scalar.copy(out=dst, in_=src)
+            nc.scalar.copy(out=dst, in_=src)
 
-        rw_scalar(0)
-        rw_vector(0)
+        rw_vector(0, 64, 128)
         gate(2)
-        nc.vector.quantize_mx(out=xc[:].bitcast(FP8X4), scales=xs[:], in_=gx[:])
+        qw(0)
         gate()
         b1T = keep.tile([P, 5 * E], F32, name="b1T")
         nc.vector.tensor_copy(out=b1T[:], in_=pb[:, 0 : 5 * E])
-        qw(0)
+        nc.vector.quantize_mx(out=xc[:].bitcast(FP8X4), scales=xs[:], in_=gx[:])
         gate(2)
-        mm1(0)
         rw_scalar(1)
         rw_vector(1)
-        rw2(0)
+        mm1(0)
         gate()
+        rw2(0)
         qw(1)
         gate()
         rw_scalar(2)
@@ -317,7 +401,7 @@ def tile_mblfe_pa_kernel(tc, x, noise, clean_logits, noise_pre, W1, b1, W2, b2, 
         qw2(0)
         gate()
 
-        for i in range(E):
+        for i in range(LAST):
             tanh(i)
             if i >= 2 and i - 2 < FIRST_VECTOR_GATING:
                 mul(i - 2)
@@ -325,8 +409,10 @@ def tile_mblfe_pa_kernel(tc, x, noise, clean_logits, noise_pre, W1, b1, W2, b2, 
                 rw_scalar(i + 3)
             if i >= 1:
                 yb(i - 1)
-            if i + 1 < E:
+            if i + 1 < LAST:
                 mm1(i + 1)
+            else:
+                mm1_last(0)
             if i >= 1:
                 tr(i - 1)
             rh(i)
@@ -339,16 +425,27 @@ def tile_mblfe_pa_kernel(tc, x, noise, clean_logits, noise_pre, W1, b1, W2, b2, 
             qh(i)
             gate()
             mm2(i)
-            if i + 1 < E:
-                rw2(i + 1)
+            rw2(i + 1)
             gate()
             if i + 3 < E:
                 rw_vector(i + 3)
             gate()
-            if i + 1 < E:
-                qw2(i + 1)
+            qw2(i + 1)
             gate()
-        yb(E - 1)
-        mul(E - 2)
-        tr(E - 1)
-        mul(E - 1)
+            if i == FIRST_VECTOR_GATING:
+                gb2_last()
+        tanh_last(0)
+        mm1_last(1)
+        tanh_last(1)
+        yb(LAST - 1)
+        mul(LAST - 2)
+        rh_last(0)
+        qh_last(0)
+        mm2_last(0)
+        tr(LAST - 1)
+        rh_last(1)
+        fin_last(0)
+        qh_last(1)
+        mm2_last(1)
+        mul(LAST - 1)
+        fin_last(1)

@@ -71,7 +71,6 @@ def tile_mblfe_pa_kernel(tc, x, noise, clean_logits, noise_pre, W1, b1, W2, b2, 
         nc.scalar.dma_start(out=b1raw[0:64, :], in_=b1.rearrange("e (t p) -> (e t) p", p=P))
         nc.scalar.dma_start(out=b1raw[64:80, :], in_=b2)
         b2last = keep.tile([P, L], BF16, name="b2last")
-        nc.scalar.dma_start(out=b2last[:], in_=b2[E - 1].partition_broadcast(P))
 
         load_w1(1)
         load_w2(0)
@@ -79,6 +78,7 @@ def tile_mblfe_pa_kernel(tc, x, noise, clean_logits, noise_pre, W1, b1, W2, b2, 
             load_w1(e)
             if e in (5, 9, 12):
                 load_w2((e + 1) // 4)
+        nc.sync.dma_start(out=b2last[:], in_=b2[E - 1].partition_broadcast(P))
 
         ident = keep.tile([P, P], F32, name="ident")
         make_identity(nc, ident[:])

@@ -32,7 +32,6 @@ def tile_mblfe_pa_kernel(tc, x, noise, clean_logits, noise_pre, W1, b1, W2, b2, 
         ps1 = ctx.enter_context(tc.psum_pool(name="ps1", bufs=5))
         psy = ctx.enter_context(tc.psum_pool(name="psy", bufs=1))
         ps2 = ctx.enter_context(tc.psum_pool(name="ps2", bufs=2))
-        ctx.enter_context(tc.manual_schedule())
 
         x_sb = keep.tile([P, NB * D], BF16, name="x_sb", align_bytes=64)
         w1raw = []

@@ -21,7 +21,7 @@ FIRST_VECTOR_GATING = 12
 
 
 def scalar_groups(e):
-    return 0 if e < 3 else 8
+    return 0 if e < 3 else 16
 
 
 def tile_mblfe_pa_kernel(tc, x, noise, clean_logits, noise_pre, W1, b1, W2, b2, out):
@@ -32,6 +32,7 @@ def tile_mblfe_pa_kernel(tc, x, noise, clean_logits, noise_pre, W1, b1, W2, b2, 
         ps1 = ctx.enter_context(tc.psum_pool(name="ps1", bufs=5))
         psy = ctx.enter_context(tc.psum_pool(name="psy", bufs=1))
         ps2 = ctx.enter_context(tc.psum_pool(name="ps2", bufs=2))
+        ctx.enter_context(tc.manual_schedule())
 
         x_sb = keep.tile([P, NB * D], BF16, name="x_sb", align_bytes=64)
         w1raw = []

@@ -20,8 +20,7 @@ FLOPS = 2 * E * B * D * H + 2 * E * B * H * L
 FIRST_VECTOR_GATING = 12
 
 
-def scalar_groups(e):
-    return 0 if e < 3 else 16
+PE_COLS = 256
 
 
 def tile_mblfe_pa_kernel(tc, x, noise, clean_logits, noise_pre, W1, b1, W2, b2, out):
@@ -29,9 +28,10 @@ def tile_mblfe_pa_kernel(tc, x, noise, clean_logits, noise_pre, W1, b1, W2, b2, 
     with ExitStack() as ctx:
         keep = ctx.enter_context(tc.tile_pool(name="keep", bufs=1))
         rot = ctx.enter_context(tc.tile_pool(name="rot", bufs=3))
-        ps1 = ctx.enter_context(tc.psum_pool(name="ps1", bufs=5))
+        ps1 = ctx.enter_context(tc.psum_pool(name="ps1", bufs=4))
         psy = ctx.enter_context(tc.psum_pool(name="psy", bufs=1))
         ps2 = ctx.enter_context(tc.psum_pool(name="ps2", bufs=2))
+        psw = ctx.enter_context(tc.psum_pool(name="psw", bufs=1))
         ctx.enter_context(tc.manual_schedule())
 
         x_sb = keep.tile([P, NB * D], BF16, name="x_sb", align_bytes=64)
@@ -82,6 +82,8 @@ def tile_mblfe_pa_kernel(tc, x, noise, clean_logits, noise_pre, W1, b1, W2, b2, 
 
         ident = keep.tile([P, P], F32, name="ident")
         make_identity(nc, ident[:])
+        ident_bf = keep.tile([P, P], BF16, name="ident_bf")
+        make_identity(nc, ident_bf[:])
 
         def gt(name, w=NB * E):
             return keep.tile([P, w], F32, name=name)
@@ -157,17 +159,30 @@ def tile_mblfe_pa_kernel(tc, x, noise, clean_logits, noise_pre, W1, b1, W2, b2, 
         ys = {}
         pt = {}
 
-        def rw_scalar(e):
-            g1[e] = rot.tile([P, 4 * H], BF16, name="g1", tag="g1", bufs=4, align_bytes=64)
-            k = scalar_groups(e)
-            if k > 0:
-                dst, src = views(g1[e][:], w1raw[e][:])
-                nc.scalar.copy(out=dst[:, 0:k], in_=src[:, 0:k])
+        pw = {}
 
-        def rw_vector(e, lo_group=None, hi_group=128):
-            k = scalar_groups(e) if lo_group is None else lo_group
+        def new_g1(e):
+            g1[e] = rot.tile([P, 4 * H], BF16, name="g1", tag="g1", bufs=4, align_bytes=64)
+
+        def rw_pe(e):
+            pw[e] = psw.tile([P, 4 * PE_COLS], BF16, name="pw", tag="w")
+            words = pw[e][:].rearrange("p (c j) -> p c j", j=4)
+            rows = w1raw[e][:].rearrange("p (j c) -> p c j", j=4)
+            for j in (0, 2):
+                nc.tensor.matmul(
+                    out=words[:, :, j : j + 2],
+                    lhsT=ident_bf[:],
+                    rhs=rows[:, H - PE_COLS :, j : j + 2],
+                    start=True,
+                    stop=True,
+                )
+
+        def rw_scalar(e):
+            nc.scalar.copy(out=g1[e][:, 4 * (H - PE_COLS) :], in_=pw[e][:])
+
+        def rw_vector(e, lo_group=0, hi_group=(H - PE_COLS) // 4):
             dst, src = views(g1[e][:], w1raw[e][:])
-            nc.vector.tensor_copy(out=dst[:, k:hi_group], in_=src[:, k:hi_group])
+            nc.vector.tensor_copy(out=dst[:, lo_group:hi_group], in_=src[:, lo_group:hi_group])
 
         def qw(e):
             w1c[e] = rot.tile([P, H], U32, name="w1c", tag="w1c", bufs=5, align_bytes=64)
@@ -369,7 +384,7 @@ def tile_mblfe_pa_kernel(tc, x, noise, clean_logits, noise_pre, W1, b1, W2, b2, 
                         in_=x32[:, 2 * half + m, u, :],
                         identity=ident[:],
                     )
-        rw_scalar(0)
+        new_g1(0)
         rw_vector(0, 0, 64)
         b1f = keep.tile([P, P], F32, name="b1f")
         nc.vector.tensor_copy(out=b1f[:], in_=b1raw[:])
@@ -388,6 +403,8 @@ def tile_mblfe_pa_kernel(tc, x, noise, clean_logits, noise_pre, W1, b1, W2, b2, 
         nc.vector.tensor_copy(out=b1T[:], in_=pb[:, 0 : 5 * E])
         nc.vector.quantize_mx(out=xc[:].bitcast(FP8X4), scales=xs[:], in_=gx[:])
         gate(2)
+        new_g1(1)
+        rw_pe(1)
         rw_scalar(1)
         rw_vector(1)
         mm1(0)
@@ -395,7 +412,8 @@ def tile_mblfe_pa_kernel(tc, x, noise, clean_logits, noise_pre, W1, b1, W2, b2, 
         rw2(0)
         qw(1)
         gate()
-        rw_scalar(2)
+        new_g1(2)
+        rw_pe(2)
         rw_vector(2)
         gate()
         qw2(0)
@@ -403,16 +421,20 @@ def tile_mblfe_pa_kernel(tc, x, noise, clean_logits, noise_pre, W1, b1, W2, b2, 
 
         for i in range(LAST):
             tanh(i)
+            if i == 0:
+                rw_scalar(2)
             if i >= 2 and i - 2 < FIRST_VECTOR_GATING:
                 mul(i - 2)
-            if i + 3 < E:
-                rw_scalar(i + 3)
             if i >= 1:
                 yb(i - 1)
             if i + 1 < LAST:
                 mm1(i + 1)
             else:
                 mm1_last(0)
+            if i + 3 < E:
+                new_g1(i + 3)
+                rw_pe(i + 3)
+                rw_scalar(i + 3)
             if i >= 1:
                 tr(i - 1)
             rh(i)

@@ -421,8 +421,8 @@ def tile_mblfe_pa_kernel(tc, x, noise, clean_logits, noise_pre, W1, b1, W2, b2, 
 
         for i in range(LAST):
             tanh(i)
-            if i == 0:
-                rw_scalar(2)
+            if i + 2 < E:
+                rw_scalar(i + 2)
             if i >= 2 and i - 2 < FIRST_VECTOR_GATING:
                 mul(i - 2)
             if i >= 1:
@@ -433,8 +433,6 @@ def tile_mblfe_pa_kernel(tc, x, noise, clean_logits, noise_pre, W1, b1, W2, b2, 
                 mm1_last(0)
             if i + 3 < E:
                 new_g1(i + 3)
-                rw_pe(i + 3)
-                rw_scalar(i + 3)
             if i >= 1:
                 tr(i - 1)
             rh(i)
@@ -447,6 +445,8 @@ def tile_mblfe_pa_kernel(tc, x, noise, clean_logits, noise_pre, W1, b1, W2, b2, 
             qh(i)
             gate()
             mm2(i)
+            if i + 3 < E:
+                rw_pe(i + 3)
             rw2(i + 1)
             gate()
             if i + 3 < E:

@@ -166,13 +166,13 @@ def tile_mblfe_pa_kernel(tc, x, noise, clean_logits, noise_pre, W1, b1, W2, b2, 
 
         def rw_pe(e):
             pw[e] = psw.tile([P, 4 * PE_COLS], BF16, name="pw", tag="w")
-            words = pw[e][:].rearrange("p (c j) -> p c j", j=4)
-            rows = w1raw[e][:].rearrange("p (j c) -> p c j", j=4)
+            words = pw[e][:].rearrange("p (c j) -> p j c", j=4)
+            rows = w1raw[e][:].rearrange("p (j c) -> p j c", j=4)
             for j in (0, 2):
                 nc.tensor.matmul(
-                    out=words[:, :, j : j + 2],
+                    out=words[:, j : j + 2, :],
                     lhsT=ident_bf[:],
-                    rhs=rows[:, H - PE_COLS :, j : j + 2],
+                    rhs=rows[:, j : j + 2, H - PE_COLS :],
                     start=True,
                     stop=True,
                 )

@@ -433,6 +433,7 @@ def tile_mblfe_pa_kernel(tc, x, noise, clean_logits, noise_pre, W1, b1, W2, b2, 
                 mm1_last(0)
             if i + 3 < E:
                 new_g1(i + 3)
+                rw_pe(i + 3)
             if i >= 1:
                 tr(i - 1)
             rh(i)
@@ -445,8 +446,6 @@ def tile_mblfe_pa_kernel(tc, x, noise, clean_logits, noise_pre, W1, b1, W2, b2, 
             qh(i)
             gate()
             mm2(i)
-            if i + 3 < E:
-                rw_pe(i + 3)
             rw2(i + 1)
             gate()
             if i + 3 < E:

@@ -20,6 +20,10 @@ FLOPS = 2 * E * B * D * H + 2 * E * B * H * L
 FIRST_VECTOR_GATING = 12
 
 
+def vgate(e):
+    return e % 3 > 0 and e < 13
+
+
 PE_COLS = 256
 
 
@@ -46,8 +50,8 @@ def tile_mblfe_pa_kernel(tc, x, noise, clean_logits, noise_pre, W1, b1, W2, b2, 
                 in_=W1[e].rearrange("(p j) h -> p j h", j=4)[:, :, cols],
             )
 
-        load_w1_half(0, 0)
         nc.sync.dma_start(out=x_sb[:], in_=x.rearrange("(p n) d -> p (n d)", n=NB))
+        load_w1_half(0, 0)
         load_w1_half(0, 1)
         w2raw = keep.tile([P, E * 4 * L], BF16, name="w2raw", align_bytes=64)
 
@@ -180,14 +184,23 @@ def tile_mblfe_pa_kernel(tc, x, noise, clean_logits, noise_pre, W1, b1, W2, b2, 
         def rw_scalar(e):
             nc.scalar.copy(out=g1[e][:, 4 * (H - PE_COLS) :], in_=pw[e][:])
 
+        def rw_strided(e, lo_group, hi_group):
+            dst, src = views(g1[e][:], w1raw[e][:])
+            nc.scalar.copy(out=dst[:, lo_group:hi_group], in_=src[:, lo_group:hi_group])
+
         def rw_vector(e, lo_group=0, hi_group=(H - PE_COLS) // 4):
             dst, src = views(g1[e][:], w1raw[e][:])
             nc.vector.tensor_copy(out=dst[:, lo_group:hi_group], in_=src[:, lo_group:hi_group])
 
-        def qw(e):
-            w1c[e] = rot.tile([P, H], U32, name="w1c", tag="w1c", bufs=5, align_bytes=64)
-            w1s[e] = rot.tile([P, H], U8, name="w1s", tag="w1s", bufs=5, align_bytes=64)
-            nc.vector.quantize_mx(out=w1c[e][:].bitcast(FP8X4), scales=w1s[e][:], in_=g1[e][:])
+        def qw(e, lo_col=0, hi_col=H):
+            if lo_col == 0:
+                w1c[e] = rot.tile([P, H], U32, name="w1c", tag="w1c", bufs=5, align_bytes=64)
+                w1s[e] = rot.tile([P, H], U8, name="w1s", tag="w1s", bufs=5, align_bytes=64)
+            nc.vector.quantize_mx(
+                out=w1c[e][:, lo_col:hi_col].bitcast(FP8X4),
+                scales=w1s[e][:, lo_col:hi_col],
+                in_=g1[e][:, 4 * lo_col : 4 * hi_col],
+            )
 
         def rw2(e):
             g3[e] = rot.tile([P, 4 * L], BF16, name="g3", tag="g3", bufs=5, align_bytes=64)
@@ -198,9 +211,10 @@ def tile_mblfe_pa_kernel(tc, x, noise, clean_logits, noise_pre, W1, b1, W2, b2, 
             cols = slice(e * L, (e + 1) * L)
             nc.vector.quantize_mx(out=w2c[:, cols].bitcast(FP8X4), scales=w2s[:, cols], in_=g3[e][:])
 
-        def mm1(e):
-            pz[e] = []
-            for t in range(4):
+        def mm1(e, tiles=(0, 1, 2, 3)):
+            if tiles[0] == 0:
+                pz[e] = []
+            for t in tiles:
                 z = ps1.tile([P, 512], F32, name="z", tag="s1")
                 cols = slice(t * P, (t + 1) * P)
                 nc.tensor.matmul_mx(
@@ -214,9 +228,10 @@ def tile_mblfe_pa_kernel(tc, x, noise, clean_logits, noise_pre, W1, b1, W2, b2, 
                 )
                 pz[e].append(z)
 
-        def tanh(e):
-            hT[e] = rot.tile([P, 4 * B], BF16, name="hT", tag="hT", bufs=3, align_bytes=64)
-            for t in range(4):
+        def tanh(e, tiles=(0, 1, 2, 3)):
+            if tiles[0] == 0:
+                hT[e] = rot.tile([P, 4 * B], BF16, name="hT", tag="hT", bufs=3, align_bytes=64)
+            for t in tiles:
                 nc.scalar.activation(
                     out=hT[e][:, t * B : (t + 1) * B],
                     in_=pz[e][t][:],
@@ -265,7 +280,7 @@ def tile_mblfe_pa_kernel(tc, x, noise, clean_logits, noise_pre, W1, b1, W2, b2, 
 
         def mul(e):
             ecols = slice(e * L, (e + 1) * L)
-            if e >= FIRST_VECTOR_GATING:
+            if vgate(e):
                 nc.vector.tensor_tensor(
                     out=o3[:, :, ecols],
                     in0=pt[e][:].rearrange("p (n l) -> p n l", n=NB),
@@ -298,29 +313,12 @@ def tile_mblfe_pa_kernel(tc, x, noise, clean_logits, noise_pre, W1, b1, W2, b2, 
                     op0=ALU.mult,
                 )
 
-        def mm1_last(h):
-            pz[(LAST, h)] = []
-            for t in range(4):
-                z = ps1.tile([P, 512], F32, name="z", tag="s1")
-                cols = slice(t * P, (t + 1) * P)
-                bcols = slice(h * HB, (h + 1) * HB)
-                nc.tensor.matmul_mx(
-                    out=z[:, 0:HB],
-                    lhsT=w1c[LAST][:, cols].bitcast(FP8X4),
-                    lhsT_scale=w1s[LAST][:, cols],
-                    rhs=xc[:, bcols].bitcast(FP8X4),
-                    rhs_scale=xs[:, bcols],
-                    start=True,
-                    stop=True,
-                )
-                pz[(LAST, h)].append(z)
-
         def tanh_last(h):
             hT[(LAST, h)] = rot.tile([P, 4 * HB], BF16, name="hT", tag="hT", bufs=3, align_bytes=64)
             for t in range(4):
                 nc.scalar.activation(
                     out=hT[(LAST, h)][:, t * HB : (t + 1) * HB],
-                    in_=pz[(LAST, h)][t][:, 0:HB],
+                    in_=pz[LAST][t][:, h * HB : (h + 1) * HB],
                     func=ACT.Tanh,
                     bias=b1T[:, 4 * LAST + t : 4 * LAST + t + 1],
                     scale=1.0,
@@ -384,53 +382,51 @@ def tile_mblfe_pa_kernel(tc, x, noise, clean_logits, noise_pre, W1, b1, W2, b2, 
                         in_=x32[:, 2 * half + m, u, :],
                         identity=ident[:],
                     )
-        new_g1(0)
-        rw_vector(0, 0, 64)
-        b1f = keep.tile([P, P], F32, name="b1f")
-        nc.vector.tensor_copy(out=b1f[:], in_=b1raw[:])
-        pb = ps2.tile([P, 512], F32, name="pb", tag="s2")
-        nc.tensor.transpose(out=pb[:, 0:P], in_=b1f[:], identity=ident[:])
-        for half in range(2):
+        pb = ps2.tile([P, P], BF16, name="pb", tag="s2")
+        nc.tensor.transpose(out=pb[:], in_=b1raw[:], identity=ident_bf[:])
+
+        def x_out(half):
             dst = gx32[:, half * 512 : (half + 1) * 512].rearrange("p (m b u) -> p m b u", m=2, u=2)
             src = xt[half][:].rearrange("p (m u b) -> p m b u", m=2, u=2)
             nc.scalar.copy(out=dst, in_=src)
 
-        rw_vector(0, 64, 128)
+        new_g1(0)
         gate(2)
-        qw(0)
-        gate()
+        rw_vector(0, 0, 64)
+        x_out(0)
+        x_out(1)
+        qw(0, 0, 256)
+        rw_vector(0, 64, 128)
         b1T = keep.tile([P, 5 * E], F32, name="b1T")
         nc.vector.tensor_copy(out=b1T[:], in_=pb[:, 0 : 5 * E])
         nc.vector.quantize_mx(out=xc[:].bitcast(FP8X4), scales=xs[:], in_=gx[:])
-        gate(2)
+        mm1(0, (0, 1))
         new_g1(1)
-        rw_pe(1)
-        rw_scalar(1)
-        rw_vector(1)
-        mm1(0)
-        gate()
-        rw2(0)
-        qw(1)
-        gate()
+        rw_strided(1, 64, 128)
+        qw(0, 256, 512)
+        mm1(0, (2, 3))
         new_g1(2)
         rw_pe(2)
+        gate()
+        rw_vector(1)
+        gate()
+        tanh(0)
+        qw(1)
+        gate()
+        rw2(0)
         rw_vector(2)
-        gate()
         qw2(0)
-        gate()
 
         for i in range(LAST):
-            tanh(i)
+            if i > 0:
+                tanh(i)
             if i + 2 < E:
                 rw_scalar(i + 2)
-            if i >= 2 and i - 2 < FIRST_VECTOR_GATING:
+            if i >= 2 and not vgate(i - 2):
                 mul(i - 2)
             if i >= 1:
                 yb(i - 1)
-            if i + 1 < LAST:
-                mm1(i + 1)
-            else:
-                mm1_last(0)
+            mm1(i + 1)
             if i + 3 < E:
                 new_g1(i + 3)
                 rw_pe(i + 3)
@@ -441,7 +437,7 @@ def tile_mblfe_pa_kernel(tc, x, noise, clean_logits, noise_pre, W1, b1, W2, b2, 
             if i + 2 < E:
                 qw(i + 2)
             gate()
-            if i >= 2 and i - 2 >= FIRST_VECTOR_GATING:
+            if i >= 2 and vgate(i - 2):
                 mul(i - 2)
             qh(i)
             gate()
@@ -456,7 +452,6 @@ def tile_mblfe_pa_kernel(tc, x, noise, clean_logits, noise_pre, W1, b1, W2, b2, 
             if i == FIRST_VECTOR_GATING:
                 gb2_last()
         tanh_last(0)
-        mm1_last(1)
         tanh_last(1)
         yb(LAST - 1)
         mul(LAST - 2)

@@ -21,7 +21,7 @@ FIRST_VECTOR_GATING = 12
 
 
 def vgate(e):
-    return e % 3 > 0 and e < 13
+    return e % 2 > 0 and e < 13
 
 
 PE_COLS = 256
@@ -77,8 +77,9 @@ def tile_mblfe_pa_kernel(tc, x, noise, clean_logits, noise_pre, W1, b1, W2, b2, 
         b2last = keep.tile([P, L], BF16, name="b2last")
 
         load_w1(1)
+        load_w1(2)
         load_w2(0)
-        for e in range(2, E):
+        for e in range(3, E):
             load_w1(e)
             if e in (5, 9, 12):
                 load_w2((e + 1) // 4)
@@ -391,30 +392,33 @@ def tile_mblfe_pa_kernel(tc, x, noise, clean_logits, noise_pre, W1, b1, W2, b2, 
             nc.scalar.copy(out=dst, in_=src)
 
         new_g1(0)
-        gate(2)
+        gate(3)
         rw_vector(0, 0, 64)
         x_out(0)
         x_out(1)
+        gate()
         qw(0, 0, 256)
+        gate()
         rw_vector(0, 64, 128)
         b1T = keep.tile([P, 5 * E], F32, name="b1T")
         nc.vector.tensor_copy(out=b1T[:], in_=pb[:, 0 : 5 * E])
         nc.vector.quantize_mx(out=xc[:].bitcast(FP8X4), scales=xs[:], in_=gx[:])
         mm1(0, (0, 1))
         new_g1(1)
-        rw_strided(1, 64, 128)
+        rw_strided(1, 96, 128)
         qw(0, 256, 512)
         mm1(0, (2, 3))
         new_g1(2)
         rw_pe(2)
         gate()
-        rw_vector(1)
+        rw_vector(1, 0, 96)
         gate()
         tanh(0)
         qw(1)
         gate()
-        rw2(0)
         rw_vector(2)
+        rw2(0)
+        gate()
         qw2(0)
 
         for i in range(LAST):

@@ -1,3 +1,4 @@
+import math
 from contextlib import ExitStack
 
 import concourse.mybir as mybir
@@ -21,7 +22,7 @@ FIRST_VECTOR_GATING = 12
 
 
 def vgate(e):
-    return e % 2 > 0 and e < 13
+    return e % 2 > 0
 
 
 PE_COLS = 256
@@ -99,6 +100,11 @@ def tile_mblfe_pa_kernel(tc, x, noise, clean_logits, noise_pre, W1, b1, W2, b2, 
         def bc(t):
             return t[:].unsqueeze(2).to_broadcast([P, NB, E])
 
+        ones = gt("ones")
+        euler = gt("euler")
+        nc.gpsimd.memset(ones[:], 1.0)
+        nc.gpsimd.tensor_scalar(out=euler[:], in0=ones[:], scalar1=math.e, scalar2=None, op0=ALU.mult)
+        warm = gt("warm", 1)
         nabs = gt("nabs")
         eu = gt("eu")
         lg = gt("lg")
@@ -365,8 +371,9 @@ def tile_mblfe_pa_kernel(tc, x, noise, clean_logits, noise_pre, W1, b1, W2, b2, 
             nc.sync.dma_start(out=out_v[:, 2 * h : 2 * h + 2, lcols], in_=o3[:, 2 * h : 2 * h + 2, lcols])
 
         nc.vector.scalar_tensor_tensor(out=nabs[:], in0=np_in[:], scalar=-1.0, in1=np_in[:], op0=ALU.mult, op1=ALU.min)
-        nc.scalar.activation(out=eu[:], in_=nabs[:], func=ACT.Exp)
+        nc.gpsimd.tensor_tensor(out=eu[:], in0=euler[:], in1=nabs[:], op=ALU.pow)
         nc.scalar.activation(out=lg[:], in_=eu[:], func=ACT.Ln, bias=1.0, scale=1.0)
+        nc.scalar.activation(out=warm[:], in_=eu[:, 0:1], func=ACT.Tanh)
 
         x32 = x_sb[:].bitcast(F32).rearrange("p (n q u) -> p n u q", n=NB, u=2)
         gx = keep.tile([P, 4 * B], BF16, name="gx", align_bytes=64)
@@ -399,7 +406,8 @@ def tile_mblfe_pa_kernel(tc, x, noise, clean_logits, noise_pre, W1, b1, W2, b2, 
         gate()
         qw(0, 0, 256)
         gate()
-        rw_vector(0, 64, 128)
+        rw_strided(0, 112, 128)
+        rw_vector(0, 64, 112)
         b1T = keep.tile([P, 5 * E], F32, name="b1T")
         nc.vector.tensor_copy(out=b1T[:], in_=pb[:, 0 : 5 * E])
         nc.vector.quantize_mx(out=xc[:].bitcast(FP8X4), scales=xs[:], in_=gx[:])
@@ -443,10 +451,13 @@ def tile_mblfe_pa_kernel(tc, x, noise, clean_logits, noise_pre, W1, b1, W2, b2, 
             gate()
             if i >= 2 and vgate(i - 2):
                 mul(i - 2)
+            if i + 2 >= E:
+                rw2(i + 1)
             qh(i)
             gate()
             mm2(i)
-            rw2(i + 1)
+            if i + 2 < E:
+                rw2(i + 1)
             gate()
             if i + 3 < E:
                 rw_vector(i + 3)

@@ -1,4 +1,3 @@
-import math
 from contextlib import ExitStack
 
 import concourse.mybir as mybir
@@ -100,11 +99,6 @@ def tile_mblfe_pa_kernel(tc, x, noise, clean_logits, noise_pre, W1, b1, W2, b2, 
         def bc(t):
             return t[:].unsqueeze(2).to_broadcast([P, NB, E])
 
-        ones = gt("ones")
-        euler = gt("euler")
-        nc.gpsimd.memset(ones[:], 1.0)
-        nc.gpsimd.tensor_scalar(out=euler[:], in0=ones[:], scalar1=math.e, scalar2=None, op0=ALU.mult)
-        warm = gt("warm", 1)
         nabs = gt("nabs")
         eu = gt("eu")
         lg = gt("lg")
@@ -371,9 +365,8 @@ def tile_mblfe_pa_kernel(tc, x, noise, clean_logits, noise_pre, W1, b1, W2, b2, 
             nc.sync.dma_start(out=out_v[:, 2 * h : 2 * h + 2, lcols], in_=o3[:, 2 * h : 2 * h + 2, lcols])
 
         nc.vector.scalar_tensor_tensor(out=nabs[:], in0=np_in[:], scalar=-1.0, in1=np_in[:], op0=ALU.mult, op1=ALU.min)
-        nc.gpsimd.tensor_tensor(out=eu[:], in0=euler[:], in1=nabs[:], op=ALU.pow)
+        nc.scalar.activation(out=eu[:], in_=nabs[:], func=ACT.Exp)
         nc.scalar.activation(out=lg[:], in_=eu[:], func=ACT.Ln, bias=1.0, scale=1.0)
-        nc.scalar.activation(out=warm[:], in_=eu[:, 0:1], func=ACT.Tanh)
 
         x32 = x_sb[:].bitcast(F32).rearrange("p (n q u) -> p n u q", n=NB, u=2)
         gx = keep.tile([P, 4 * B], BF16, name="gx", align_bytes=64)
@@ -398,28 +391,34 @@ def tile_mblfe_pa_kernel(tc, x, noise, clean_logits, noise_pre, W1, b1, W2, b2, 
             src = xt[half][:].rearrange("p (m u b) -> p m b u", m=2, u=2)
             nc.scalar.copy(out=dst, in_=src)
 
+        def x_out_v(half):
+            dst = gx32[:, half * 512 : (half + 1) * 512].rearrange("p (m b u) -> p m b u", m=2, u=2)
+            src = xt[half][:].rearrange("p (m u b) -> p m b u", m=2, u=2)
+            nc.vector.tensor_copy(out=dst, in_=src)
+
         new_g1(0)
-        gate(3)
-        rw_vector(0, 0, 64)
+        gate(0)
         x_out(0)
+        rw_vector(0, 0, 64)
         x_out(1)
         gate()
         qw(0, 0, 256)
         gate()
         rw_strided(0, 112, 128)
         rw_vector(0, 64, 112)
+        gate()
         b1T = keep.tile([P, 5 * E], F32, name="b1T")
         nc.vector.tensor_copy(out=b1T[:], in_=pb[:, 0 : 5 * E])
         nc.vector.quantize_mx(out=xc[:].bitcast(FP8X4), scales=xs[:], in_=gx[:])
+        gate()
         mm1(0, (0, 1))
         new_g1(1)
-        rw_strided(1, 96, 128)
         qw(0, 256, 512)
         mm1(0, (2, 3))
         new_g1(2)
         rw_pe(2)
         gate()
-        rw_vector(1, 0, 96)
+        rw_vector(1, 0, 128)
         gate()
         tanh(0)
         qw(1)

@@ -468,8 +468,8 @@ def tile_mblfe_pa_kernel(tc, x, noise, clean_logits, noise_pre, W1, b1, W2, b2, 
         tanh_last(0)
         tanh_last(1)
         yb(LAST - 1)
-        mul(LAST - 2)
         rh_last(0)
+        mul(LAST - 2)
         qh_last(0)
         mm2_last(0)
         tr(LAST - 1)

from contextlib import ExitStack

import concourse.mybir as mybir
from concourse.masks import make_identity

F32 = mybir.dt.float32
BF16 = mybir.dt.bfloat16
U32 = mybir.dt.uint32
U8 = mybir.dt.uint8
FP8X4 = mybir.dt.float8_e4m3fn_x4
ACT = mybir.ActivationFunctionType
ALU = mybir.AluOpType
AX = mybir.AxisListType

P = 128
B, D, E, H, L = 512, 512, 16, 512, 128
NB = B // P
FLOPS = 2 * E * B * D * H + 2 * E * B * H * L

FIRST_VECTOR_GATING = 12


def vgate(e):
    return e % 2 > 0


PE_COLS = 256


def tile_mblfe_pa_kernel(tc, x, noise, clean_logits, noise_pre, W1, b1, W2, b2, out):
    nc = tc.nc
    with ExitStack() as ctx:
        keep = ctx.enter_context(tc.tile_pool(name="keep", bufs=1))
        rot = ctx.enter_context(tc.tile_pool(name="rot", bufs=3))
        ps1 = ctx.enter_context(tc.psum_pool(name="ps1", bufs=4))
        psy = ctx.enter_context(tc.psum_pool(name="psy", bufs=1))
        ps2 = ctx.enter_context(tc.psum_pool(name="ps2", bufs=2))
        psw = ctx.enter_context(tc.psum_pool(name="psw", bufs=1))
        ctx.enter_context(tc.manual_schedule())

        x_sb = keep.tile([P, NB * D], BF16, name="x_sb", align_bytes=64)
        w1raw = []
        for e in range(E):
            w1raw.append(keep.tile([P, 4 * H], BF16, name="w1raw%d" % e, align_bytes=64))

        def load_w1_half(e, k):
            cols = slice(k * (H // 2), (k + 1) * (H // 2))
            nc.sync.dma_start(
                out=w1raw[e][:].rearrange("p (j h) -> p j h", j=4)[:, :, cols],
                in_=W1[e].rearrange("(p j) h -> p j h", j=4)[:, :, cols],
            )

        nc.sync.dma_start(out=x_sb[:], in_=x.rearrange("(p n) d -> p (n d)", n=NB))
        load_w1_half(0, 0)
        load_w1_half(0, 1)
        w2raw = keep.tile([P, E * 4 * L], BF16, name="w2raw", align_bytes=64)

        def load_w1(e):
            nc.sync.dma_start(out=w1raw[e][:], in_=W1[e].rearrange("(p j) h -> p (j h)", j=4))

        def load_w2(q):
            nc.sync.dma_start(
                out=w2raw[:, q * 2048 : (q + 1) * 2048].rearrange("p (e t l) -> p e t l", e=4, t=4),
                in_=W2[4 * q : 4 * q + 4].rearrange("e (t p) l -> p e t l", p=P),
            )

        np_in = keep.tile([P, NB * E], BF16, name="np_in")
        no_in = keep.tile([P, NB * E], BF16, name="no_in")
        cl_in = keep.tile([P, NB * E], BF16, name="cl_in")
        nc.scalar.dma_start(out=np_in[:], in_=noise_pre.rearrange("(p n) e -> p (n e)", n=NB))
        nc.scalar.dma_start(out=no_in[:], in_=noise.rearrange("(p n) e -> p (n e)", n=NB))
        nc.scalar.dma_start(out=cl_in[:], in_=clean_logits.rearrange("(p n) e -> p (n e)", n=NB))
        b1raw = keep.tile([P, P], BF16, name="b1raw")
        nc.vector.memset(b1raw[:], 0.0)
        nc.scalar.dma_start(out=b1raw[0:64, :], in_=b1.rearrange("e (t p) -> (e t) p", p=P))
        nc.scalar.dma_start(out=b1raw[64:80, :], in_=b2)
        b2last = keep.tile([P, L], BF16, name="b2last")

        load_w1(1)
        load_w1(2)
        load_w2(0)
        for e in range(3, E):
            load_w1(e)
            if e in (5, 9, 12):
                load_w2((e + 1) // 4)
        nc.sync.dma_start(out=b2last[:], in_=b2[E - 1].partition_broadcast(P))

        ident = keep.tile([P, P], F32, name="ident")
        make_identity(nc, ident[:])
        ident_bf = keep.tile([P, P], BF16, name="ident_bf")
        make_identity(nc, ident_bf[:])

        def gt(name, w=NB * E):
            return keep.tile([P, w], F32, name=name)

        def v3(t):
            return t[:].rearrange("p (n e) -> p n e", n=NB)

        def bc(t):
            return t[:].unsqueeze(2).to_broadcast([P, NB, E])

        nabs = gt("nabs")
        eu = gt("eu")
        lg = gt("lg")
        sp = gt("sp")
        nz = gt("nz")
        lo = gt("lo")
        mx = gt("mx", NB)
        ls = gt("ls")
        ex = gt("ex")
        sm = gt("sm", NB)
        rs = gt("rs", NB)
        pr = gt("pr")
        gq = gt("gq")
        gs = gt("gs", NB)
        rg = gt("rg", NB)
        g = gt("g")

        gate_steps = [
            lambda: nc.vector.scalar_tensor_tensor(out=sp[:], in0=np_in[:], scalar=0.0, in1=lg[:], op0=ALU.max, op1=ALU.add),
            lambda: nc.vector.scalar_tensor_tensor(out=nz[:], in0=sp[:], scalar=0.01, in1=no_in[:], op0=ALU.add, op1=ALU.mult),
            lambda: nc.vector.tensor_tensor(out=lo[:], in0=nz[:], in1=cl_in[:], op=ALU.add),
            lambda: nc.vector.tensor_reduce(out=mx[:], in_=v3(lo), axis=AX.X, op=ALU.max),
            lambda: nc.vector.tensor_tensor(out=v3(ls), in0=v3(lo), in1=bc(mx), op=ALU.subtract),
            lambda: nc.vector.tensor_reduce(out=sm[:], in_=v3(ex), axis=AX.X, op=ALU.add),
            lambda: nc.vector.reciprocal(out=rs[:], in_=sm[:]),
            lambda: nc.vector.tensor_tensor(out=v3(pr), in0=v3(ex), in1=bc(rs), op=ALU.mult),
            lambda: nc.vector.scalar_tensor_tensor(out=gq[:], in0=pr[:], scalar=1.0 / E - 1e-8, in1=pr[:], op0=ALU.is_ge, op1=ALU.mult),
            lambda: nc.vector.tensor_reduce(out=gs[:], in_=v3(gq), axis=AX.X, op=ALU.add),
            lambda: nc.vector.reciprocal(out=rg[:], in_=gs[:]),
            lambda: nc.vector.tensor_tensor(out=v3(g), in0=v3(gq), in1=bc(rg), op=ALU.mult),
        ]
        taken = [0]

        def gate(count=1):
            for k in range(count):
                if taken[0] < len(gate_steps):
                    gate_steps[taken[0]]()
                    taken[0] = taken[0] + 1
                    if taken[0] == 5:
                        nc.scalar.activation(out=ex[:], in_=ls[:], func=ACT.Exp)

        o = keep.tile([P, NB * E * L], F32, name="o")
        o3 = o[:].rearrange("p (n c) -> p n c", n=NB)
        out_v = out.rearrange("(p n) e l -> p n (e l)", n=NB)
        w2c = keep.tile([P, E * L], U32, name="w2c", align_bytes=64)
        w2s = keep.tile([P, E * L], U8, name="w2s", align_bytes=64)

        def views(dst2d, src2d):
            src = src2d.rearrange("p (j c i) -> p c j i", j=4, i=4)
            dst = dst2d.rearrange("p (c i j) -> p c j i", i=4, j=4)
            return dst, src

        g1 = {}
        w1c = {}
        w1s = {}
        g3 = {}
        hT = {}
        g2 = {}
        hc = {}
        hs = {}
        pz = {}
        py = {}
        ys = {}
        pt = {}

        pw = {}

        def new_g1(e):
            g1[e] = rot.tile([P, 4 * H], BF16, name="g1", tag="g1", bufs=4, align_bytes=64)

        def rw_pe(e):
            pw[e] = psw.tile([P, 4 * PE_COLS], BF16, name="pw", tag="w")
            words = pw[e][:].rearrange("p (c j) -> p j c", j=4)
            rows = w1raw[e][:].rearrange("p (j c) -> p j c", j=4)
            for j in (0, 2):
                nc.tensor.matmul(
                    out=words[:, j : j + 2, :],
                    lhsT=ident_bf[:],
                    rhs=rows[:, j : j + 2, H - PE_COLS :],
                    start=True,
                    stop=True,
                )

        def rw_scalar(e):
            nc.scalar.copy(out=g1[e][:, 4 * (H - PE_COLS) :], in_=pw[e][:])

        def rw_strided(e, lo_group, hi_group):
            dst, src = views(g1[e][:], w1raw[e][:])
            nc.scalar.copy(out=dst[:, lo_group:hi_group], in_=src[:, lo_group:hi_group])

        def rw_vector(e, lo_group=0, hi_group=(H - PE_COLS) // 4):
            dst, src = views(g1[e][:], w1raw[e][:])
            nc.vector.tensor_copy(out=dst[:, lo_group:hi_group], in_=src[:, lo_group:hi_group])

        def qw(e, lo_col=0, hi_col=H):
            if lo_col == 0:
                w1c[e] = rot.tile([P, H], U32, name="w1c", tag="w1c", bufs=5, align_bytes=64)
                w1s[e] = rot.tile([P, H], U8, name="w1s", tag="w1s", bufs=5, align_bytes=64)
            nc.vector.quantize_mx(
                out=w1c[e][:, lo_col:hi_col].bitcast(FP8X4),
                scales=w1s[e][:, lo_col:hi_col],
                in_=g1[e][:, 4 * lo_col : 4 * hi_col],
            )

        def rw2(e):
            g3[e] = rot.tile([P, 4 * L], BF16, name="g3", tag="g3", bufs=5, align_bytes=64)
            dst, src = views(g3[e][:], w2raw[:, e * 512 : (e + 1) * 512])
            nc.vector.tensor_copy(out=dst, in_=src)

        def qw2(e):
            cols = slice(e * L, (e + 1) * L)
            nc.vector.quantize_mx(out=w2c[:, cols].bitcast(FP8X4), scales=w2s[:, cols], in_=g3[e][:])

        def mm1(e, tiles=(0, 1, 2, 3)):
            if tiles[0] == 0:
                pz[e] = []
            for t in tiles:
                z = ps1.tile([P, 512], F32, name="z", tag="s1")
                cols = slice(t * P, (t + 1) * P)
                nc.tensor.matmul_mx(
                    out=z[:],
                    lhsT=w1c[e][:, cols].bitcast(FP8X4),
                    lhsT_scale=w1s[e][:, cols],
                    rhs=xc[:].bitcast(FP8X4),
                    rhs_scale=xs[:],
                    start=True,
                    stop=True,
                )
                pz[e].append(z)

        def tanh(e, tiles=(0, 1, 2, 3)):
            if tiles[0] == 0:
                hT[e] = rot.tile([P, 4 * B], BF16, name="hT", tag="hT", bufs=3, align_bytes=64)
            for t in tiles:
                nc.scalar.activation(
                    out=hT[e][:, t * B : (t + 1) * B],
                    in_=pz[e][t][:],
                    func=ACT.Tanh,
                    bias=b1T[:, 4 * e + t : 4 * e + t + 1],
                    scale=1.0,
                )

        def rh(e):
            g2[e] = rot.tile([P, 4 * B], BF16, name="g2", tag="g2", bufs=3, align_bytes=64)
            dst, src = views(g2[e][:], hT[e][:])
            nc.vector.tensor_copy(out=dst, in_=src)

        def qh(e):
            hc[e] = rot.tile([P, B], U32, name="hc", tag="hc", bufs=3, align_bytes=64)
            hs[e] = rot.tile([P, B], U8, name="hs", tag="hs", bufs=3, align_bytes=64)
            nc.vector.quantize_mx(out=hc[e][:].bitcast(FP8X4), scales=hs[e][:], in_=g2[e][:])

        def mm2(e):
            py[e] = psy.tile([P, 512], F32, name="y", tag="y")
            wcols = slice(e * L, (e + 1) * L)
            nc.tensor.matmul_mx(
                out=py[e][:],
                lhsT=w2c[:, wcols].bitcast(FP8X4),
                lhsT_scale=w2s[:, wcols],
                rhs=hc[e][:].bitcast(FP8X4),
                rhs_scale=hs[e][:],
                start=True,
                stop=True,
            )

        def yb(e):
            ys[e] = rot.tile([P, B], F32, name="ys", tag="ys", bufs=2)
            nc.scalar.activation(
                out=ys[e][:], in_=py[e][:], func=ACT.Identity, bias=b1T[:, 4 * E + e : 4 * E + e + 1], scale=1.0
            )

        def tr(e):
            pt[e] = ps2.tile([P, 512], F32, name="pt", tag="s2")
            for n in range(NB):
                cols = slice(n * P, (n + 1) * P)
                nc.tensor.transpose(out=pt[e][:, cols], in_=ys[e][:, cols], identity=ident[:])

        store_after = {3: 0, 7: 4, 11: 8, 13: 12, 14: 14}
        g3d = g[:].rearrange("p (n e) -> p n e", n=NB)

        def mul(e):
            ecols = slice(e * L, (e + 1) * L)
            if vgate(e):
                nc.vector.tensor_tensor(
                    out=o3[:, :, ecols],
                    in0=pt[e][:].rearrange("p (n l) -> p n l", n=NB),
                    in1=g3d[:, :, e : e + 1].to_broadcast([P, NB, L]),
                    op=ALU.mult,
                )
            else:
                for n in range(NB):
                    nc.scalar.activation(
                        out=o3[:, n, ecols],
                        in_=pt[e][:, n * P : (n + 1) * P],
                        func=ACT.Copy,
                        scale=g[:, n * E + e : n * E + e + 1],
                    )
            if e in store_after:
                cols = slice(store_after[e] * L, (e + 1) * L)
                nc.sync.dma_start(out=out_v[:, :, cols], in_=o3[:, :, cols])

        LAST = E - 1
        lcols = slice(LAST * L, (LAST + 1) * L)
        HB = B // 2

        def gb2_last():
            for n in range(NB):
                nc.vector.tensor_scalar(
                    out=o3[:, n, lcols],
                    in0=b2last[:],
                    scalar1=g[:, n * E + LAST : n * E + LAST + 1],
                    scalar2=None,
                    op0=ALU.mult,
                )

        def tanh_last(h):
            hT[(LAST, h)] = rot.tile([P, 4 * HB], BF16, name="hT", tag="hT", bufs=3, align_bytes=64)
            for t in range(4):
                nc.scalar.activation(
                    out=hT[(LAST, h)][:, t * HB : (t + 1) * HB],
                    in_=pz[LAST][t][:, h * HB : (h + 1) * HB],
                    func=ACT.Tanh,
                    bias=b1T[:, 4 * LAST + t : 4 * LAST + t + 1],
                    scale=1.0,
                )

        def rh_last(h):
            g2[(LAST, h)] = rot.tile([P, 4 * HB], BF16, name="g2", tag="g2", bufs=3, align_bytes=64)
            dst, src = views(g2[(LAST, h)][:], hT[(LAST, h)][:])
            nc.vector.tensor_copy(out=dst, in_=src)

        def qh_last(h):
            hc[(LAST, h)] = rot.tile([P, HB], U32, name="hc", tag="hc", bufs=3, align_bytes=64)
            hs[(LAST, h)] = rot.tile([P, HB], U8, name="hs", tag="hs", bufs=3, align_bytes=64)
            nc.vector.quantize_mx(
                out=hc[(LAST, h)][:].bitcast(FP8X4), scales=hs[(LAST, h)][:], in_=g2[(LAST, h)][:]
            )

        def mm2_last(h):
            py[(LAST, h)] = ps2.tile([P, 512], F32, name="yl", tag="s2")
            for m in range(2):
                cols = slice(m * P, (m + 1) * P)
                nc.tensor.matmul_mx(
                    out=py[(LAST, h)][:, cols],
                    lhsT=hc[(LAST, h)][:, cols].bitcast(FP8X4),
                    lhsT_scale=hs[(LAST, h)][:, cols],
                    rhs=w2c[:, lcols].bitcast(FP8X4),
                    rhs_scale=w2s[:, lcols],
                    start=True,
                    stop=True,
                )

        def fin_last(h):
            for m in range(2):
                n = 2 * h + m
                nc.vector.scalar_tensor_tensor(
                    out=o3[:, n, lcols],
                    in0=py[(LAST, h)][:, m * P : (m + 1) * P],
                    scalar=g[:, n * E + LAST : n * E + LAST + 1],
                    in1=o3[:, n, lcols],
                    op0=ALU.mult,
                    op1=ALU.add,
                )
            nc.sync.dma_start(out=out_v[:, 2 * h : 2 * h + 2, lcols], in_=o3[:, 2 * h : 2 * h + 2, lcols])

        nc.vector.scalar_tensor_tensor(out=nabs[:], in0=np_in[:], scalar=-1.0, in1=np_in[:], op0=ALU.mult, op1=ALU.min)
        nc.scalar.activation(out=eu[:], in_=nabs[:], func=ACT.Exp)
        nc.scalar.activation(out=lg[:], in_=eu[:], func=ACT.Ln, bias=1.0, scale=1.0)

        x32 = x_sb[:].bitcast(F32).rearrange("p (n q u) -> p n u q", n=NB, u=2)
        gx = keep.tile([P, 4 * B], BF16, name="gx", align_bytes=64)
        gx32 = gx[:].bitcast(F32)
        xc = keep.tile([P, B], U32, name="xc", align_bytes=64)
        xs = keep.tile([P, B], U8, name="xs", align_bytes=64)
        xt = []
        for half in range(2):
            xt.append(ps1.tile([P, 512], F32, name="xt", tag="s1"))
            for m in range(2):
                for u in range(2):
                    nc.tensor.transpose(
                        out=xt[half][:, (2 * m + u) * P : (2 * m + u + 1) * P],
                        in_=x32[:, 2 * half + m, u, :],
                        identity=ident[:],
                    )
        pb = ps2.tile([P, P], BF16, name="pb", tag="s2")
        nc.tensor.transpose(out=pb[:], in_=b1raw[:], identity=ident_bf[:])

        def x_out(half):
            dst = gx32[:, half * 512 : (half + 1) * 512].rearrange("p (m b u) -> p m b u", m=2, u=2)
            src = xt[half][:].rearrange("p (m u b) -> p m b u", m=2, u=2)
            nc.scalar.copy(out=dst, in_=src)

        def x_out_v(half):
            dst = gx32[:, half * 512 : (half + 1) * 512].rearrange("p (m b u) -> p m b u", m=2, u=2)
            src = xt[half][:].rearrange("p (m u b) -> p m b u", m=2, u=2)
            nc.vector.tensor_copy(out=dst, in_=src)

        new_g1(0)
        gate(0)
        x_out(0)
        rw_vector(0, 0, 64)
        x_out(1)
        gate()
        qw(0, 0, 256)
        gate()
        rw_strided(0, 112, 128)
        rw_vector(0, 64, 112)
        gate()
        b1T = keep.tile([P, 5 * E], F32, name="b1T")
        nc.vector.tensor_copy(out=b1T[:], in_=pb[:, 0 : 5 * E])
        nc.vector.quantize_mx(out=xc[:].bitcast(FP8X4), scales=xs[:], in_=gx[:])
        gate()
        mm1(0, (0, 1))
        new_g1(1)
        qw(0, 256, 512)
        mm1(0, (2, 3))
        new_g1(2)
        rw_pe(2)
        gate()
        rw_vector(1, 0, 128)
        gate()
        tanh(0)
        qw(1)
        gate()
        rw_vector(2)
        rw2(0)
        gate()
        qw2(0)

        for i in range(LAST):
            if i > 0:
                tanh(i)
            if i + 2 < E:
                rw_scalar(i + 2)
            if i >= 2 and not vgate(i - 2):
                mul(i - 2)
            if i >= 1:
                yb(i - 1)
            mm1(i + 1)
            if i + 3 < E:
                new_g1(i + 3)
                rw_pe(i + 3)
            if i >= 1:
                tr(i - 1)
            rh(i)
            gate()
            if i + 2 < E:
                qw(i + 2)
            gate()
            if i >= 2 and vgate(i - 2):
                mul(i - 2)
            if i + 2 >= E:
                rw2(i + 1)
            qh(i)
            gate()
            mm2(i)
            if i + 2 < E:
                rw2(i + 1)
            gate()
            if i + 3 < E:
                rw_vector(i + 3)
            gate()
            qw2(i + 1)
            gate()
            if i == FIRST_VECTOR_GATING:
                gb2_last()
        tanh_last(0)
        tanh_last(1)
        yb(LAST - 1)
        rh_last(0)
        mul(LAST - 2)
        qh_last(0)
        mm2_last(0)
        tr(LAST - 1)
        rh_last(1)
        fin_last(0)
        qh_last(1)
        mm2_last(1)
        mul(LAST - 1)
        fin_last(1)
